import numpy as np
import ml_dtypes


def mxq(x, axis, fmt="e4m3"):
    dtype, down = {"e4m3": (ml_dtypes.float8_e4m3fn, 7), "e5m2": (ml_dtypes.float8_e5m2, 14)}[fmt]
    v = np.moveaxis(np.asarray(x, np.float32).astype(ml_dtypes.bfloat16).astype(np.float64), axis, -1)
    blocks = v.reshape(v.shape[:-1] + (-1, 32))
    amax = np.abs(blocks).max(-1, keepdims=True)
    byte = np.maximum(np.where(amax > 0, np.frexp(amax)[1] - 1 + 127, 0) - down, 1)
    scale = np.exp2(byte - 127.0)
    codes = (blocks / scale).astype(np.float32).astype(dtype).astype(np.float64)
    return np.moveaxis((codes * scale).reshape(v.shape), -1, axis)


WIDE = False


def mx_kscale(k):
    if not WIDE:
        return np.ones(k)
    levels = np.array([10, -10, 5, -5, 0])
    a = np.random.permutation(np.resize(levels, k // 512 * 4)).reshape(k // 512, 4)
    idx = np.arange(k)
    return np.exp2(a[idx // 512, idx % 128 // 32])


BF16 = ml_dtypes.bfloat16


def bf(x):
    return np.asarray(x, np.float32).astype(BF16)


def f64(x):
    return np.asarray(x).astype(np.float64)


B, S, D_IN, D_OUT, R = 4, 2048, 512, 128, 512


def setup_inputs():
    t = mx_kscale(R)
    sk = t[np.arange(D_IN) % R]
    so = t[np.arange(D_OUT) * R // D_OUT]
    m_v = sk[:, None] == t[None, :]
    m_u = so[:, None] == t[None, :]
    g = R / m_u.sum(1)
    return {"x": bf(np.random.standard_normal((B, S, D_IN))),
            "U_latent": bf(np.random.standard_normal((D_OUT, R)) * 0.05 * m_u),
            "V_latent": bf(np.random.standard_normal((D_IN, R)) * 0.05 * m_v),
            "s1": bf(np.random.uniform(1.0, 4.0, D_OUT) / np.sqrt(R) * g / so),
            "s2": bf(np.random.uniform(0.25, 1.0, D_IN) / np.sqrt(D_IN) * sk),
            "bias": bf(np.random.standard_normal(D_OUT) * 0.5)}


def reference(x, U_latent, V_latent, s1, s2, bias):
    u_sign = np.sign(f64(U_latent))
    v_sign = np.sign(f64(V_latent))
    a = f64(x) * f64(s2)
    h = mxq(a, 2, "e4m3") @ mxq(v_sign, 0, "e4m3")
    z = mxq(h, 2, "e4m3") @ mxq(u_sign, 1, "e4m3").T
    return z * f64(s1) + f64(bias)

@@ -1,0 +1,224 @@
+from contextlib import ExitStack
+
+import concourse.mybir as mybir
+from concourse.masks import make_identity
+
+BF16 = mybir.dt.bfloat16
+F32 = mybir.dt.float32
+U32 = mybir.dt.uint32
+U8 = mybir.dt.uint8
+FP8X4 = mybir.dt.float8_e4m3fn_x4
+ALU = mybir.AluOpType
+
+P = 128
+PACK = 4
+HALVES = 2
+TOKENS = 4 * 2048
+D_IN = 512
+R = 512
+D_OUT = 128
+TILES = 4
+ROUNDS = TOKENS // (TILES * P)
+BANK_TILES = 2
+
+FLOPS = 2 * TOKENS * D_IN * R + 2 * TOKENS * R * D_OUT
+
+
+def sign_of(nc, pool, values, width, name):
+    positive = pool.tile([P, width], BF16, name=name + "_positive")
+    negative = pool.tile([P, width], BF16, name=name + "_negative")
+    sign = pool.tile([P, width], BF16, name=name + "_sign")
+    nc.vector.tensor_scalar(out=positive[:], in0=values, scalar1=0.0, scalar2=None, op0=ALU.is_gt)
+    nc.vector.tensor_scalar(out=negative[:], in0=values, scalar1=0.0, scalar2=None, op0=ALU.is_lt)
+    nc.vector.tensor_tensor(out=sign[:], in0=positive[:], in1=negative[:], op=ALU.subtract)
+    return sign
+
+
+def tile_binaryfactoredlinear_pa_t_kernel(tc, x, U_latent, V_latent, s1, s2, bias, out):
+    nc = tc.nc
+    x_rounds = x.flatten_outer_dims().rearrange("(c p j) k -> c p j k", p=P, j=TILES)
+    out_rounds = out.flatten_outer_dims().rearrange("(c p j) o -> c p j o", p=P, j=TILES)
+
+    with ExitStack() as ctx:
+        const = ctx.enter_context(tc.tile_pool(name="const", bufs=1))
+        x_pool = ctx.enter_context(tc.tile_pool(name="x_pool", bufs=ROUNDS))
+        work = ctx.enter_context(tc.tile_pool(name="work", bufs=3))
+        psum_x = ctx.enter_context(tc.psum_pool(name="psum_x", bufs=2))
+        psum_h = ctx.enter_context(tc.psum_pool(name="psum_h", bufs=4))
+        psum_z = ctx.enter_context(tc.psum_pool(name="psum_z", bufs=2))
+        ctx.enter_context(tc.manual_schedule())
+
+        v_raw = const.tile([P, PACK, R], BF16)
+        nc.sync.dma_start(
+            out=v_raw[:].rearrange("p (u e) r -> p u (e r)", u=HALVES),
+            in_=V_latent.rearrange("(u p e) r -> p u (e r)", u=HALVES, e=2),
+        )
+        x_tiles = []
+        for c in range(ROUNDS):
+            x_sb = x_pool.tile([P, TILES, D_IN], BF16)
+            nc.sync.dma_start(out=x_sb[:], in_=x_rounds[c])
+            x_tiles.append(x_sb)
+        s2_word = const.tile([P, PACK], BF16)
+        nc.scalar.dma_start(
+            out=s2_word[:].rearrange("p (u e) -> p u e", u=HALVES),
+            in_=s2.rearrange("(u p e) -> p u e", u=HALVES, e=2),
+        )
+        u_raw = const.tile([P, R], BF16)
+        nc.scalar.dma_start(out=u_raw[:], in_=U_latent)
+        s1_bf = const.tile([P, D_OUT], BF16)
+        nc.scalar.dma_start(out=s1_bf[:], in_=s1.partition_broadcast(P))
+        bias_bf = const.tile([P, D_OUT], BF16)
+        nc.scalar.dma_start(out=bias_bf[:], in_=bias.partition_broadcast(P))
+
+        identity = const.tile([P, P], F32)
+        make_identity(nc, identity[:])
+        s1_rows = const.tile([P, D_OUT], F32)
+        nc.gpsimd.tensor_copy(out=s1_rows[:], in_=s1_bf[:])
+        bias_rows = const.tile([P, D_OUT], F32)
+        nc.gpsimd.tensor_copy(out=bias_rows[:], in_=bias_bf[:])
+
+        x_banks = {}
+        a_grouped = {}
+        a_mx = {}
+        h_grouped = {}
+        h_mx = {}
+        z_banks = {}
+
+        def transpose_x(c):
+            x_words = x_tiles[c][:].bitcast(F32)
+            x_banks[c] = []
+            for b in range(TILES // BANK_TILES):
+                xt = psum_x.tile([P, HALVES, BANK_TILES * P], F32)
+                for i in range(BANK_TILES):
+                    for u in range(HALVES):
+                        nc.tensor.transpose(
+                            xt[:, u, i * P : (i + 1) * P],
+                            x_words[:, b * BANK_TILES + i, u * P : (u + 1) * P],
+                            identity[:],
+                        )
+                x_banks[c].append(xt)
+
+        def scale_x(c):
+            a_bf = work.tile([P, TILES * P, HALVES, 2], BF16, align_bytes=64)
+            bank_tokens = BANK_TILES * P
+            for b, xt in enumerate(x_banks[c]):
+                nc.vector.tensor_tensor(
+                    out=a_bf[:, b * bank_tokens : (b + 1) * bank_tokens, :, :],
+                    in0=xt[:].bitcast(BF16).rearrange("p u (n e) -> p n u e", e=2),
+                    in1=s2_word[:]
+                    .rearrange("p (u e) -> p u e", u=HALVES)
+                    .unsqueeze(1)
+                    .to_broadcast([P, bank_tokens, HALVES, 2]),
+                    op=ALU.mult,
+                )
+            a_grouped[c] = a_bf
+
+        def quantise(grouped_flat, name):
+            codes = work.tile([P, TILES * P], U32, align_bytes=64, name=name + "_codes")
+            scales = work.tile([P, TILES * P], U8, align_bytes=64, name=name + "_scales")
+            nc.vector.quantize_mx(out=codes[:].bitcast(FP8X4), scales=scales[:], in_=grouped_flat)
+            return codes, scales
+
+        def first_matmul(c):
+            codes, scales = a_mx[c]
+            h_bf = work.tile([P, TILES, P, PACK], BF16, align_bytes=64)
+            for j in range(TILES):
+                tokens = slice(j * P, (j + 1) * P)
+                hT = psum_h.tile([P, PACK, P], F32)
+                for s in range(PACK):
+                    columns = slice(s * P, (s + 1) * P)
+                    nc.tensor.matmul_mx(
+                        out=hT[:, s, :],
+                        lhsT=v_codes[:, columns].bitcast(FP8X4),
+                        lhsT_scale=v_scales[:, columns],
+                        rhs=codes[:, tokens].bitcast(FP8X4),
+                        rhs_scale=scales[:, tokens],
+                        start=True,
+                        stop=True,
+                    )
+                nc.scalar.copy(out=h_bf[:, j, :, :], in_=hT[:].rearrange("m s n -> m n s"))
+            h_grouped[c] = h_bf
+
+        def second_matmul(c):
+            codes, scales = h_mx[c]
+            z = psum_z.tile([P, TILES, D_OUT], F32)
+            for j in range(TILES):
+                tokens = slice(j * P, (j + 1) * P)
+                nc.tensor.matmul_mx(
+                    out=z[:, j, :],
+                    lhsT=codes[:, tokens].bitcast(FP8X4),
+                    lhsT_scale=scales[:, tokens],
+                    rhs=u_codes[:].bitcast(FP8X4),
+                    rhs_scale=u_scales[:],
+                    start=True,
+                    stop=True,
+                )
+            z_banks[c] = z
+
+        def finish(c):
+            scaled = work.tile([P, TILES, D_OUT], F32)
+            nc.vector.tensor_tensor(
+                out=scaled[:],
+                in0=z_banks[c][:],
+                in1=s1_rows[:].unsqueeze(1).to_broadcast([P, TILES, D_OUT]),
+                op=ALU.mult,
+            )
+            result = work.tile([P, TILES, D_OUT], F32)
+            nc.gpsimd.tensor_tensor(
+                out=result[:],
+                in0=scaled[:],
+                in1=bias_rows[:].unsqueeze(1).to_broadcast([P, TILES, D_OUT]),
+                op=ALU.add,
+            )
+            nc.sync.dma_start(out=out_rounds[c], in_=result[:])
+
+        v_sign = sign_of(nc, const, v_raw[:].rearrange("p t r -> p (t r)"), PACK * R, "v")
+        u_sign = sign_of(nc, const, u_raw[:], R, "u")
+        v_grouped = const.tile([P, PACK, P, PACK], BF16, align_bytes=64)
+        nc.scalar.copy(
+            out=v_grouped[:],
+            in_=v_sign[:].rearrange("p (t m s) -> p s m t", t=PACK, s=PACK),
+        )
+
+        transpose_x(0)
+        scale_x(0)
+        a_mx[0] = quantise(a_grouped[0][:].rearrange("p n u e -> p (n u e)"), "a")
+
+        v_codes = const.tile([P, R], U32, align_bytes=64)
+        v_scales = const.tile([P, R], U8, align_bytes=64)
+        nc.vector.quantize_mx(
+            out=v_codes[:].bitcast(FP8X4),
+            scales=v_scales[:],
+            in_=v_grouped[:].rearrange("p s m t -> p (s m t)"),
+        )
+
+        u_words = u_sign[:].bitcast(F32).rearrange("o (m u) -> o u m", u=HALVES)
+        uT = psum_x.tile([P, HALVES, D_OUT], F32, tag="xt")
+        for u in range(HALVES):
+            nc.tensor.transpose(uT[:, u, :], u_words[:, u, :], identity[:])
+        u_grouped = const.tile([P, D_OUT * PACK], BF16, align_bytes=64)
+        nc.scalar.copy(
+            out=u_grouped[:].bitcast(F32).rearrange("m (o u) -> m o u", u=HALVES),
+            in_=uT[:].rearrange("m u o -> m o u"),
+        )
+        u_codes = const.tile([P, D_OUT], U32, align_bytes=64)
+        u_scales = const.tile([P, D_OUT], U8, align_bytes=64)
+        nc.vector.quantize_mx(out=u_codes[:].bitcast(FP8X4), scales=u_scales[:], in_=u_grouped[:])
+
+        def live(c):
+            return 0 <= c < ROUNDS
+
+        for n in range(ROUNDS + 3):
+            if live(n - 3):
+                finish(n - 3)
+            if live(n + 1):
+                transpose_x(n + 1)
+                scale_x(n + 1)
+            if live(n - 1):
+                h_mx[n - 1] = quantise(h_grouped[n - 1][:].rearrange("m j n s -> m (j n s)"), "h")
+            if live(n + 1):
+                a_mx[n + 1] = quantise(a_grouped[n + 1][:].rearrange("p n u e -> p (n u e)"), "a")
+            if live(n - 2):
+                second_matmul(n - 2)
+            if live(n):
+                first_matmul(n)

@@ -9,6 +9,7 @@ U32 = mybir.dt.uint32
 U8 = mybir.dt.uint8
 FP8X4 = mybir.dt.float8_e4m3fn_x4
 ALU = mybir.AluOpType
+ACT = mybir.ActivationFunctionType
 
 P = 128
 PACK = 4
@@ -45,7 +46,8 @@ def tile_binaryfactoredlinear_pa_t_kernel(tc, x, U_latent, V_latent, s1, s2, bia
         work = ctx.enter_context(tc.tile_pool(name="work", bufs=3))
         psum_x = ctx.enter_context(tc.psum_pool(name="psum_x", bufs=2))
         psum_h = ctx.enter_context(tc.psum_pool(name="psum_h", bufs=4))
-        psum_z = ctx.enter_context(tc.psum_pool(name="psum_z", bufs=2))
+        psum_z = ctx.enter_context(tc.psum_pool(name="psum_z", bufs=1))
+        psum_o = ctx.enter_context(tc.psum_pool(name="psum_o", bufs=1))
         ctx.enter_context(tc.manual_schedule())
 
         v_raw = const.tile([P, PACK, R], BF16)
@@ -65,24 +67,25 @@ def tile_binaryfactoredlinear_pa_t_kernel(tc, x, U_latent, V_latent, s1, s2, bia
         )
         u_raw = const.tile([P, R], BF16)
         nc.scalar.dma_start(out=u_raw[:], in_=U_latent)
-        s1_bf = const.tile([P, D_OUT], BF16)
-        nc.scalar.dma_start(out=s1_bf[:], in_=s1.partition_broadcast(P))
-        bias_bf = const.tile([P, D_OUT], BF16)
-        nc.scalar.dma_start(out=bias_bf[:], in_=bias.partition_broadcast(P))
+        s1_bf = const.tile([P, 1], BF16)
+        nc.scalar.dma_start(out=s1_bf[:], in_=s1.rearrange("(o one) -> o one", one=1))
+        bias_bf = const.tile([P, 1], BF16)
+        nc.scalar.dma_start(out=bias_bf[:], in_=bias.rearrange("(o one) -> o one", one=1))
 
         identity = const.tile([P, P], F32)
         make_identity(nc, identity[:])
-        s1_rows = const.tile([P, D_OUT], F32)
-        nc.gpsimd.tensor_copy(out=s1_rows[:], in_=s1_bf[:])
-        bias_rows = const.tile([P, D_OUT], F32)
-        nc.gpsimd.tensor_copy(out=bias_rows[:], in_=bias_bf[:])
+        s1_col = const.tile([P, 1], F32)
+        nc.gpsimd.tensor_copy(out=s1_col[:], in_=s1_bf[:])
+        bias_col = const.tile([P, 1], F32)
+        nc.gpsimd.tensor_copy(out=bias_col[:], in_=bias_bf[:])
 
         x_banks = {}
         a_grouped = {}
         a_mx = {}
         h_grouped = {}
         h_mx = {}
-        z_banks = {}
+        outT = {}
+        out_banks = {}
 
         def transpose_x(c):
             x_words = x_tiles[c][:].bitcast(F32)
@@ -141,35 +144,31 @@ def tile_binaryfactoredlinear_pa_t_kernel(tc, x, U_latent, V_latent, s1, s2, bia
 
         def second_matmul(c):
             codes, scales = h_mx[c]
-            z = psum_z.tile([P, TILES, D_OUT], F32)
-            for j in range(TILES):
-                tokens = slice(j * P, (j + 1) * P)
-                nc.tensor.matmul_mx(
-                    out=z[:, j, :],
-                    lhsT=codes[:, tokens].bitcast(FP8X4),
-                    lhsT_scale=scales[:, tokens],
-                    rhs=u_codes[:].bitcast(FP8X4),
-                    rhs_scale=u_scales[:],
-                    start=True,
-                    stop=True,
-                )
-            z_banks[c] = z
+            zT = psum_z.tile([P, TILES * P], F32)
+            nc.tensor.matmul_mx(
+                out=zT[:],
+                lhsT=u_codes[:].bitcast(FP8X4),
+                lhsT_scale=u_scales[:],
+                rhs=codes[:].bitcast(FP8X4),
+                rhs_scale=scales[:],
+                start=True,
+                stop=True,
+            )
+            oT = work.tile([P, TILES * P], F32)
+            nc.scalar.activation(
+                out=oT[:], in_=zT[:], func=ACT.Identity, scale=s1_col[:, 0:1], bias=bias_col[:, 0:1]
+            )
+            outT[c] = oT
 
-        def finish(c):
-            scaled = work.tile([P, TILES, D_OUT], F32)
-            nc.vector.tensor_tensor(
-                out=scaled[:],
-                in0=z_banks[c][:],
-                in1=s1_rows[:].unsqueeze(1).to_broadcast([P, TILES, D_OUT]),
-                op=ALU.mult,
-            )
+        def transpose_out(c):
+            o_bank = psum_o.tile([P, TILES, D_OUT], F32)
+            for j in range(TILES):
+                nc.tensor.transpose(o_bank[:, j, :], outT[c][:, j * P : (j + 1) * P], identity[:])
+            out_banks[c] = o_bank
+
+        def store_out(c):
             result = work.tile([P, TILES, D_OUT], F32)
-            nc.gpsimd.tensor_tensor(
-                out=result[:],
-                in0=scaled[:],
-                in1=bias_rows[:].unsqueeze(1).to_broadcast([P, TILES, D_OUT]),
-                op=ALU.add,
-            )
+            nc.vector.tensor_copy(out=result[:], in_=out_banks[c][:])
             nc.sync.dma_start(out=out_rounds[c], in_=result[:])
 
         v_sign = sign_of(nc, const, v_raw[:].rearrange("p t r -> p (t r)"), PACK * R, "v")
@@ -209,11 +208,14 @@ def tile_binaryfactoredlinear_pa_t_kernel(tc, x, U_latent, V_latent, s1, s2, bia
             return 0 <= c < ROUNDS
 
         for n in range(ROUNDS + 3):
-            if live(n - 3):
-                finish(n - 3)
             if live(n + 1):
                 transpose_x(n + 1)
+            if live(n - 3):
+                transpose_out(n - 3)
+            if live(n + 1):
                 scale_x(n + 1)
+            if live(n - 3):
+                store_out(n - 3)
             if live(n - 1):
                 h_mx[n - 1] = quantise(h_grouped[n - 1][:].rearrange("m j n s -> m (j n s)"), "h")
             if live(n + 1):

@@ -20,6 +20,7 @@ R = 512
 D_OUT = 128
 TILES = 4
 ROUNDS = TOKENS // (TILES * P)
+SHARED_ROUNDS = 2
 BANK_TILES = 2
 
 FLOPS = 2 * TOKENS * D_IN * R + 2 * TOKENS * R * D_OUT
@@ -75,9 +76,9 @@ def tile_binaryfactoredlinear_pa_t_kernel(tc, x, U_latent, V_latent, s1, s2, bia
         identity = const.tile([P, P], F32)
         make_identity(nc, identity[:])
         s1_col = const.tile([P, 1], F32)
-        nc.gpsimd.tensor_copy(out=s1_col[:], in_=s1_bf[:])
+        nc.scalar.activation(out=s1_col[:], in_=s1_bf[:], func=ACT.Identity)
         bias_col = const.tile([P, 1], F32)
-        nc.gpsimd.tensor_copy(out=bias_col[:], in_=bias_bf[:])
+        nc.scalar.activation(out=bias_col[:], in_=bias_bf[:], func=ACT.Identity)
 
         x_banks = {}
         a_grouped = {}
@@ -139,7 +140,10 @@ def tile_binaryfactoredlinear_pa_t_kernel(tc, x, U_latent, V_latent, s1, s2, bia
                         start=True,
                         stop=True,
                     )
-                nc.scalar.copy(out=h_bf[:, j, :, :], in_=hT[:].rearrange("m s n -> m n s"))
+                if c >= ROUNDS - SHARED_ROUNDS and j % 2 == 1:
+                    nc.vector.tensor_copy(out=h_bf[:, j, :, :], in_=hT[:].rearrange("m s n -> m n s"))
+                else:
+                    nc.scalar.copy(out=h_bf[:, j, :, :], in_=hT[:].rearrange("m s n -> m n s"))
             h_grouped[c] = h_bf
 
         def second_matmul(c):
@@ -171,26 +175,7 @@ def tile_binaryfactoredlinear_pa_t_kernel(tc, x, U_latent, V_latent, s1, s2, bia
             nc.vector.tensor_copy(out=result[:], in_=out_banks[c][:])
             nc.sync.dma_start(out=out_rounds[c], in_=result[:])
 
-        v_sign = sign_of(nc, const, v_raw[:].rearrange("p t r -> p (t r)"), PACK * R, "v")
         u_sign = sign_of(nc, const, u_raw[:], R, "u")
-        v_grouped = const.tile([P, PACK, P, PACK], BF16, align_bytes=64)
-        nc.scalar.copy(
-            out=v_grouped[:],
-            in_=v_sign[:].rearrange("p (t m s) -> p s m t", t=PACK, s=PACK),
-        )
-
-        transpose_x(0)
-        scale_x(0)
-        a_mx[0] = quantise(a_grouped[0][:].rearrange("p n u e -> p (n u e)"), "a")
-
-        v_codes = const.tile([P, R], U32, align_bytes=64)
-        v_scales = const.tile([P, R], U8, align_bytes=64)
-        nc.vector.quantize_mx(
-            out=v_codes[:].bitcast(FP8X4),
-            scales=v_scales[:],
-            in_=v_grouped[:].rearrange("p s m t -> p (s m t)"),
-        )
-
         u_words = u_sign[:].bitcast(F32).rearrange("o (m u) -> o u m", u=HALVES)
         uT = psum_x.tile([P, HALVES, D_OUT], F32, tag="xt")
         for u in range(HALVES):
@@ -200,6 +185,23 @@ def tile_binaryfactoredlinear_pa_t_kernel(tc, x, U_latent, V_latent, s1, s2, bia
             out=u_grouped[:].bitcast(F32).rearrange("m (o u) -> m o u", u=HALVES),
             in_=uT[:].rearrange("m u o -> m o u"),
         )
+
+        v_sign = sign_of(nc, const, v_raw[:].rearrange("p t r -> p (t r)"), PACK * R, "v")
+        v_columns = v_sign[:].rearrange("p (t m s) -> p s m t", t=PACK, s=PACK)
+        v_grouped = const.tile([P, PACK, P, PACK], BF16, align_bytes=64)
+        nc.scalar.copy(out=v_grouped[:, 0:2, :, :], in_=v_columns[:, 0:2, :, :])
+        nc.vector.tensor_copy(out=v_grouped[:, 2:4, :, :], in_=v_columns[:, 2:4, :, :])
+
+        transpose_x(0)
+        scale_x(0)
+        v_codes = const.tile([P, R], U32, align_bytes=64)
+        v_scales = const.tile([P, R], U8, align_bytes=64)
+        nc.vector.quantize_mx(
+            out=v_codes[:].bitcast(FP8X4),
+            scales=v_scales[:],
+            in_=v_grouped[:].rearrange("p s m t -> p (s m t)"),
+        )
+        a_mx[0] = quantise(a_grouped[0][:].rearrange("p n u e -> p (n u e)"), "a")
         u_codes = const.tile([P, D_OUT], U32, align_bytes=64)
         u_scales = const.tile([P, D_OUT], U8, align_bytes=64)
         nc.vector.quantize_mx(out=u_codes[:].bitcast(FP8X4), scales=u_scales[:], in_=u_grouped[:])

@@ -26,16 +26,6 @@ BANK_TILES = 2
 FLOPS = 2 * TOKENS * D_IN * R + 2 * TOKENS * R * D_OUT
 
 
-def sign_of(nc, pool, values, width, name):
-    positive = pool.tile([P, width], BF16, name=name + "_positive")
-    negative = pool.tile([P, width], BF16, name=name + "_negative")
-    sign = pool.tile([P, width], BF16, name=name + "_sign")
-    nc.vector.tensor_scalar(out=positive[:], in0=values, scalar1=0.0, scalar2=None, op0=ALU.is_gt)
-    nc.vector.tensor_scalar(out=negative[:], in0=values, scalar1=0.0, scalar2=None, op0=ALU.is_lt)
-    nc.vector.tensor_tensor(out=sign[:], in0=positive[:], in1=negative[:], op=ALU.subtract)
-    return sign
-
-
 def tile_binaryfactoredlinear_pa_t_kernel(tc, x, U_latent, V_latent, s1, s2, bias, out):
     nc = tc.nc
     x_rounds = x.flatten_outer_dims().rearrange("(c p j) k -> c p j k", p=P, j=TILES)
@@ -51,6 +41,8 @@ def tile_binaryfactoredlinear_pa_t_kernel(tc, x, U_latent, V_latent, s1, s2, bia
         psum_o = ctx.enter_context(tc.psum_pool(name="psum_o", bufs=1))
         ctx.enter_context(tc.manual_schedule())
 
+        u_raw = const.tile([P, R], BF16)
+        nc.sync.dma_start(out=u_raw[:], in_=U_latent)
         v_raw = const.tile([P, PACK, R], BF16)
         nc.sync.dma_start(
             out=v_raw[:].rearrange("p (u e) r -> p u (e r)", u=HALVES),
@@ -66,8 +58,6 @@ def tile_binaryfactoredlinear_pa_t_kernel(tc, x, U_latent, V_latent, s1, s2, bia
             out=s2_word[:].rearrange("p (u e) -> p u e", u=HALVES),
             in_=s2.rearrange("(u p e) -> p u e", u=HALVES, e=2),
         )
-        u_raw = const.tile([P, R], BF16)
-        nc.scalar.dma_start(out=u_raw[:], in_=U_latent)
         s1_bf = const.tile([P, 1], BF16)
         nc.scalar.dma_start(out=s1_bf[:], in_=s1.rearrange("(o one) -> o one", one=1))
         bias_bf = const.tile([P, 1], BF16)
@@ -175,25 +165,24 @@ def tile_binaryfactoredlinear_pa_t_kernel(tc, x, U_latent, V_latent, s1, s2, bia
             nc.vector.tensor_copy(out=result[:], in_=out_banks[c][:])
             nc.sync.dma_start(out=out_rounds[c], in_=result[:])
 
-        u_sign = sign_of(nc, const, u_raw[:], R, "u")
-        u_words = u_sign[:].bitcast(F32).rearrange("o (m u) -> o u m", u=HALVES)
-        uT = psum_x.tile([P, HALVES, D_OUT], F32, tag="xt")
+        u_words = u_raw[:].bitcast(F32).rearrange("o (m u) -> o u m", u=HALVES)
+        uT = psum_o.tile([P, HALVES, D_OUT], F32, tag="o_bank")
         for u in range(HALVES):
             nc.tensor.transpose(uT[:, u, :], u_words[:, u, :], identity[:])
-        u_grouped = const.tile([P, D_OUT * PACK], BF16, align_bytes=64)
-        nc.scalar.copy(
-            out=u_grouped[:].bitcast(F32).rearrange("m (o u) -> m o u", u=HALVES),
-            in_=uT[:].rearrange("m u o -> m o u"),
-        )
-
-        v_sign = sign_of(nc, const, v_raw[:].rearrange("p t r -> p (t r)"), PACK * R, "v")
-        v_columns = v_sign[:].rearrange("p (t m s) -> p s m t", t=PACK, s=PACK)
         v_grouped = const.tile([P, PACK, P, PACK], BF16, align_bytes=64)
-        nc.scalar.copy(out=v_grouped[:, 0:2, :, :], in_=v_columns[:, 0:2, :, :])
-        nc.vector.tensor_copy(out=v_grouped[:, 2:4, :, :], in_=v_columns[:, 2:4, :, :])
+        nc.scalar.activation(
+            out=v_grouped[:], in_=v_raw[:].rearrange("p t (m s) -> p s m t", s=PACK), func=ACT.Sign
+        )
+        u_grouped = const.tile([P, D_OUT, HALVES, 2], BF16, align_bytes=64)
+        nc.scalar.activation(
+            out=u_grouped[:],
+            in_=uT[:].bitcast(BF16).rearrange("m u (o e) -> m o u e", e=2),
+            func=ACT.Sign,
+        )
 
         transpose_x(0)
         scale_x(0)
+        a_mx[0] = quantise(a_grouped[0][:].rearrange("p n u e -> p (n u e)"), "a")
         v_codes = const.tile([P, R], U32, align_bytes=64)
         v_scales = const.tile([P, R], U8, align_bytes=64)
         nc.vector.quantize_mx(
@@ -201,10 +190,13 @@ def tile_binaryfactoredlinear_pa_t_kernel(tc, x, U_latent, V_latent, s1, s2, bia
             scales=v_scales[:],
             in_=v_grouped[:].rearrange("p s m t -> p (s m t)"),
         )
-        a_mx[0] = quantise(a_grouped[0][:].rearrange("p n u e -> p (n u e)"), "a")
         u_codes = const.tile([P, D_OUT], U32, align_bytes=64)
         u_scales = const.tile([P, D_OUT], U8, align_bytes=64)
-        nc.vector.quantize_mx(out=u_codes[:].bitcast(FP8X4), scales=u_scales[:], in_=u_grouped[:])
+        nc.vector.quantize_mx(
+            out=u_codes[:].bitcast(FP8X4),
+            scales=u_scales[:],
+            in_=u_grouped[:].rearrange("m o u e -> m (o u e)"),
+        )
 
         def live(c):
             return 0 <= c < ROUNDS

@@ -18,9 +18,9 @@ TOKENS = 4 * 2048
 D_IN = 512
 R = 512
 D_OUT = 128
-TILES = 4
-ROUNDS = TOKENS // (TILES * P)
-SHARED_ROUNDS = 2
+ROUND_TILES = [2] + [4] * 15 + [2]
+ROUNDS = len(ROUND_TILES)
+SHARED_ROUNDS = 1
 BANK_TILES = 2
 
 FLOPS = 2 * TOKENS * D_IN * R + 2 * TOKENS * R * D_OUT
@@ -28,8 +28,16 @@ FLOPS = 2 * TOKENS * D_IN * R + 2 * TOKENS * R * D_OUT
 
 def tile_binaryfactoredlinear_pa_t_kernel(tc, x, U_latent, V_latent, s1, s2, bias, out):
     nc = tc.nc
-    x_rounds = x.flatten_outer_dims().rearrange("(c p j) k -> c p j k", p=P, j=TILES)
-    out_rounds = out.flatten_outer_dims().rearrange("(c p j) o -> c p j o", p=P, j=TILES)
+    x_tokens = x.flatten_outer_dims()
+    out_tokens = out.flatten_outer_dims()
+    x_rounds = []
+    out_rounds = []
+    first_token = 0
+    for tiles in ROUND_TILES:
+        rows = slice(first_token, first_token + tiles * P)
+        x_rounds.append(x_tokens[rows, :].rearrange("(p j) k -> p j k", j=tiles))
+        out_rounds.append(out_tokens[rows, :].rearrange("(p j) o -> p j o", j=tiles))
+        first_token += tiles * P
 
     with ExitStack() as ctx:
         const = ctx.enter_context(tc.tile_pool(name="const", bufs=1))
@@ -41,18 +49,24 @@ def tile_binaryfactoredlinear_pa_t_kernel(tc, x, U_latent, V_latent, s1, s2, bia
         psum_o = ctx.enter_context(tc.psum_pool(name="psum_o", bufs=1))
         ctx.enter_context(tc.manual_schedule())
 
-        u_raw = const.tile([P, R], BF16)
-        nc.sync.dma_start(out=u_raw[:], in_=U_latent)
+        x_tiles = []
+
+        def load_x(c):
+            x_sb = x_pool.tile([P, ROUND_TILES[c], D_IN], BF16)
+            nc.sync.dma_start(out=x_sb[:], in_=x_rounds[c])
+            x_tiles.append(x_sb)
+
+        load_x(0)
         v_raw = const.tile([P, PACK, R], BF16)
         nc.sync.dma_start(
             out=v_raw[:].rearrange("p (u e) r -> p u (e r)", u=HALVES),
             in_=V_latent.rearrange("(u p e) r -> p u (e r)", u=HALVES, e=2),
         )
-        x_tiles = []
-        for c in range(ROUNDS):
-            x_sb = x_pool.tile([P, TILES, D_IN], BF16)
-            nc.sync.dma_start(out=x_sb[:], in_=x_rounds[c])
-            x_tiles.append(x_sb)
+        load_x(1)
+        u_raw = const.tile([P, R], BF16)
+        nc.sync.dma_start(out=u_raw[:], in_=U_latent)
+        for c in range(2, ROUNDS):
+            load_x(c)
         s2_word = const.tile([P, PACK], BF16)
         nc.scalar.dma_start(
             out=s2_word[:].rearrange("p (u e) -> p u e", u=HALVES),
@@ -65,10 +79,6 @@ def tile_binaryfactoredlinear_pa_t_kernel(tc, x, U_latent, V_latent, s1, s2, bia
 
         identity = const.tile([P, P], F32)
         make_identity(nc, identity[:])
-        s1_col = const.tile([P, 1], F32)
-        nc.scalar.activation(out=s1_col[:], in_=s1_bf[:], func=ACT.Identity)
-        bias_col = const.tile([P, 1], F32)
-        nc.scalar.activation(out=bias_col[:], in_=bias_bf[:], func=ACT.Identity)
 
         x_banks = {}
         a_grouped = {}
@@ -81,7 +91,7 @@ def tile_binaryfactoredlinear_pa_t_kernel(tc, x, U_latent, V_latent, s1, s2, bia
         def transpose_x(c):
             x_words = x_tiles[c][:].bitcast(F32)
             x_banks[c] = []
-            for b in range(TILES // BANK_TILES):
+            for b in range(ROUND_TILES[c] // BANK_TILES):
                 xt = psum_x.tile([P, HALVES, BANK_TILES * P], F32)
                 for i in range(BANK_TILES):
                     for u in range(HALVES):
@@ -93,7 +103,7 @@ def tile_binaryfactoredlinear_pa_t_kernel(tc, x, U_latent, V_latent, s1, s2, bia
                 x_banks[c].append(xt)
 
         def scale_x(c):
-            a_bf = work.tile([P, TILES * P, HALVES, 2], BF16, align_bytes=64)
+            a_bf = work.tile([P, ROUND_TILES[c] * P, HALVES, 2], BF16, align_bytes=64)
             bank_tokens = BANK_TILES * P
             for b, xt in enumerate(x_banks[c]):
                 nc.vector.tensor_tensor(
@@ -107,16 +117,19 @@ def tile_binaryfactoredlinear_pa_t_kernel(tc, x, U_latent, V_latent, s1, s2, bia
                 )
             a_grouped[c] = a_bf
 
-        def quantise(grouped_flat, name):
-            codes = work.tile([P, TILES * P], U32, align_bytes=64, name=name + "_codes")
-            scales = work.tile([P, TILES * P], U8, align_bytes=64, name=name + "_scales")
+        def quantise(c, grouped_flat, name):
+            codes = work.tile([P, ROUND_TILES[c] * P], U32, align_bytes=64, name=name + "_codes")
+            scales = work.tile([P, ROUND_TILES[c] * P], U8, align_bytes=64, name=name + "_scales")
             nc.vector.quantize_mx(out=codes[:].bitcast(FP8X4), scales=scales[:], in_=grouped_flat)
             return codes, scales
 
+        def quantise_a(c):
+            a_mx[c] = quantise(c, a_grouped[c][:].rearrange("p n u e -> p (n u e)"), "a")
+
         def first_matmul(c):
             codes, scales = a_mx[c]
-            h_bf = work.tile([P, TILES, P, PACK], BF16, align_bytes=64)
-            for j in range(TILES):
+            h_bf = work.tile([P, ROUND_TILES[c], P, PACK], BF16, align_bytes=64)
+            for j in range(ROUND_TILES[c]):
                 tokens = slice(j * P, (j + 1) * P)
                 hT = psum_h.tile([P, PACK, P], F32)
                 for s in range(PACK):
@@ -138,7 +151,7 @@ def tile_binaryfactoredlinear_pa_t_kernel(tc, x, U_latent, V_latent, s1, s2, bia
 
         def second_matmul(c):
             codes, scales = h_mx[c]
-            zT = psum_z.tile([P, TILES * P], F32)
+            zT = psum_z.tile([P, ROUND_TILES[c] * P], F32)
             nc.tensor.matmul_mx(
                 out=zT[:],
                 lhsT=u_codes[:].bitcast(FP8X4),
@@ -148,55 +161,65 @@ def tile_binaryfactoredlinear_pa_t_kernel(tc, x, U_latent, V_latent, s1, s2, bia
                 start=True,
                 stop=True,
             )
-            oT = work.tile([P, TILES * P], F32)
+            oT = work.tile([P, ROUND_TILES[c] * P], F32)
             nc.scalar.activation(
                 out=oT[:], in_=zT[:], func=ACT.Identity, scale=s1_col[:, 0:1], bias=bias_col[:, 0:1]
             )
             outT[c] = oT
 
         def transpose_out(c):
-            o_bank = psum_o.tile([P, TILES, D_OUT], F32)
-            for j in range(TILES):
+            o_bank = psum_o.tile([P, ROUND_TILES[c], D_OUT], F32)
+            for j in range(ROUND_TILES[c]):
                 nc.tensor.transpose(o_bank[:, j, :], outT[c][:, j * P : (j + 1) * P], identity[:])
             out_banks[c] = o_bank
 
         def store_out(c):
-            result = work.tile([P, TILES, D_OUT], F32)
+            result = work.tile([P, ROUND_TILES[c], D_OUT], F32)
             nc.vector.tensor_copy(out=result[:], in_=out_banks[c][:])
             nc.sync.dma_start(out=out_rounds[c], in_=result[:])
 
-        u_words = u_raw[:].bitcast(F32).rearrange("o (m u) -> o u m", u=HALVES)
-        uT = psum_o.tile([P, HALVES, D_OUT], F32, tag="o_bank")
-        for u in range(HALVES):
-            nc.tensor.transpose(uT[:, u, :], u_words[:, u, :], identity[:])
-        v_grouped = const.tile([P, PACK, P, PACK], BF16, align_bytes=64)
-        nc.scalar.activation(
-            out=v_grouped[:], in_=v_raw[:].rearrange("p t (m s) -> p s m t", s=PACK), func=ACT.Sign
-        )
-        u_grouped = const.tile([P, D_OUT, HALVES, 2], BF16, align_bytes=64)
-        nc.scalar.activation(
-            out=u_grouped[:],
-            in_=uT[:].bitcast(BF16).rearrange("m u (o e) -> m o u e", e=2),
-            func=ACT.Sign,
-        )
-
         transpose_x(0)
         scale_x(0)
-        a_mx[0] = quantise(a_grouped[0][:].rearrange("p n u e -> p (n u e)"), "a")
+        quantise_a(0)
+        v_grouped = const.tile([P, PACK, P, PACK], BF16, align_bytes=64)
         v_codes = const.tile([P, R], U32, align_bytes=64)
         v_scales = const.tile([P, R], U8, align_bytes=64)
-        nc.vector.quantize_mx(
-            out=v_codes[:].bitcast(FP8X4),
-            scales=v_scales[:],
-            in_=v_grouped[:].rearrange("p s m t -> p (s m t)"),
-        )
-        u_codes = const.tile([P, D_OUT], U32, align_bytes=64)
-        u_scales = const.tile([P, D_OUT], U8, align_bytes=64)
-        nc.vector.quantize_mx(
-            out=u_codes[:].bitcast(FP8X4),
-            scales=u_scales[:],
-            in_=u_grouped[:].rearrange("m o u e -> m (o u e)"),
-        )
+        for s in range(PACK):
+            columns = slice(s * P, (s + 1) * P)
+            nc.scalar.activation(
+                out=v_grouped[:, s, :, :],
+                in_=v_raw[:].rearrange("p t (m s) -> p s m t", s=PACK)[:, s, :, :],
+                func=ACT.Sign,
+            )
+            nc.vector.quantize_mx(
+                out=v_codes[:, columns].bitcast(FP8X4),
+                scales=v_scales[:, columns],
+                in_=v_grouped[:, s, :, :].rearrange("p m t -> p (m t)"),
+            )
+
+        def prepare_u():
+            u_words = u_raw[:].bitcast(F32).rearrange("o (m u) -> o u m", u=HALVES)
+            uT = psum_o.tile([P, HALVES, D_OUT], F32, tag="o_bank")
+            for u in range(HALVES):
+                nc.tensor.transpose(uT[:, u, :], u_words[:, u, :], identity[:])
+            u_grouped = const.tile([P, D_OUT, HALVES, 2], BF16, align_bytes=64)
+            nc.scalar.activation(
+                out=u_grouped[:],
+                in_=uT[:].bitcast(BF16).rearrange("m u (o e) -> m o u e", e=2),
+                func=ACT.Sign,
+            )
+            u_codes = const.tile([P, D_OUT], U32, align_bytes=64)
+            u_scales = const.tile([P, D_OUT], U8, align_bytes=64)
+            nc.vector.quantize_mx(
+                out=u_codes[:].bitcast(FP8X4),
+                scales=u_scales[:],
+                in_=u_grouped[:].rearrange("m o u e -> m (o u e)"),
+            )
+            s1_col = const.tile([P, 1], F32)
+            nc.scalar.activation(out=s1_col[:], in_=s1_bf[:], func=ACT.Identity)
+            bias_col = const.tile([P, 1], F32)
+            nc.scalar.activation(out=bias_col[:], in_=bias_bf[:], func=ACT.Identity)
+            return u_codes, u_scales, s1_col, bias_col
 
         def live(c):
             return 0 <= c < ROUNDS
@@ -211,10 +234,14 @@ def tile_binaryfactoredlinear_pa_t_kernel(tc, x, U_latent, V_latent, s1, s2, bia
             if live(n - 3):
                 store_out(n - 3)
             if live(n - 1):
-                h_mx[n - 1] = quantise(h_grouped[n - 1][:].rearrange("m j n s -> m (j n s)"), "h")
+                h_mx[n - 1] = quantise(
+                    n - 1, h_grouped[n - 1][:].rearrange("m j n s -> m (j n s)"), "h"
+                )
             if live(n + 1):
-                a_mx[n + 1] = quantise(a_grouped[n + 1][:].rearrange("p n u e -> p (n u e)"), "a")
+                quantise_a(n + 1)
             if live(n - 2):
                 second_matmul(n - 2)
             if live(n):
                 first_matmul(n)
+            if n == 0:
+                u_codes, u_scales, s1_col, bias_col = prepare_u()

@@ -20,7 +20,6 @@ R = 512
 D_OUT = 128
 ROUND_TILES = [2] + [4] * 15 + [2]
 ROUNDS = len(ROUND_TILES)
-SHARED_ROUNDS = 1
 BANK_TILES = 2
 
 FLOPS = 2 * TOKENS * D_IN * R + 2 * TOKENS * R * D_OUT
@@ -42,12 +41,25 @@ def tile_binaryfactoredlinear_pa_t_kernel(tc, x, U_latent, V_latent, s1, s2, bia
     with ExitStack() as ctx:
         const = ctx.enter_context(tc.tile_pool(name="const", bufs=1))
         x_pool = ctx.enter_context(tc.tile_pool(name="x_pool", bufs=ROUNDS))
+        result_pool = ctx.enter_context(tc.tile_pool(name="result_pool", bufs=8))
         work = ctx.enter_context(tc.tile_pool(name="work", bufs=3))
         psum_x = ctx.enter_context(tc.psum_pool(name="psum_x", bufs=2))
         psum_h = ctx.enter_context(tc.psum_pool(name="psum_h", bufs=4))
         psum_z = ctx.enter_context(tc.psum_pool(name="psum_z", bufs=1))
         psum_o = ctx.enter_context(tc.psum_pool(name="psum_o", bufs=1))
         ctx.enter_context(tc.manual_schedule())
+
+        s1_bf = const.tile([P, 1], BF16)
+        nc.scalar.dma_start(out=s1_bf[:], in_=s1.rearrange("(o one) -> o one", one=1))
+        bias_bf = const.tile([P, 1], BF16)
+        nc.scalar.dma_start(out=bias_bf[:], in_=bias.rearrange("(o one) -> o one", one=1))
+
+        rows_bf = const.tile([P, 2, D_OUT], BF16)
+        nc.gpsimd.memset(rows_bf[:], 0.0)
+        ones = const.tile([P, P], BF16)
+        nc.gpsimd.memset(ones[:], 1.0)
+        nc.scalar.dma_start(out=rows_bf[0:1, 0, :], in_=s1.rearrange("(one o) -> one o", one=1))
+        nc.scalar.dma_start(out=rows_bf[0:1, 1, :], in_=bias.rearrange("(one o) -> one o", one=1))
 
         x_tiles = []
 
@@ -56,43 +68,44 @@ def tile_binaryfactoredlinear_pa_t_kernel(tc, x, U_latent, V_latent, s1, s2, bia
             nc.sync.dma_start(out=x_sb[:], in_=x_rounds[c])
             x_tiles.append(x_sb)
 
-        load_x(0)
+        s2_word = const.tile([P, PACK], BF16)
+        nc.sync.dma_start(
+            out=s2_word[:].rearrange("p (u e) -> p u e", u=HALVES),
+            in_=s2.rearrange("(u p e) -> p u e", u=HALVES, e=2),
+        )
         v_raw = const.tile([P, PACK, R], BF16)
         nc.sync.dma_start(
             out=v_raw[:].rearrange("p (u e) r -> p u (e r)", u=HALVES),
             in_=V_latent.rearrange("(u p e) r -> p u (e r)", u=HALVES, e=2),
         )
+        load_x(0)
         load_x(1)
         u_raw = const.tile([P, R], BF16)
         nc.sync.dma_start(out=u_raw[:], in_=U_latent)
         for c in range(2, ROUNDS):
             load_x(c)
-        s2_word = const.tile([P, PACK], BF16)
-        nc.scalar.dma_start(
-            out=s2_word[:].rearrange("p (u e) -> p u e", u=HALVES),
-            in_=s2.rearrange("(u p e) -> p u e", u=HALVES, e=2),
-        )
-        s1_bf = const.tile([P, 1], BF16)
-        nc.scalar.dma_start(out=s1_bf[:], in_=s1.rearrange("(o one) -> o one", one=1))
-        bias_bf = const.tile([P, 1], BF16)
-        nc.scalar.dma_start(out=bias_bf[:], in_=bias.rearrange("(o one) -> o one", one=1))
-
         identity = const.tile([P, P], F32)
         make_identity(nc, identity[:])
 
         x_banks = {}
         a_grouped = {}
         a_mx = {}
+        h_banks = {}
         h_grouped = {}
         h_mx = {}
         outT = {}
+        z_banks = {}
+        products = {}
         out_banks = {}
+
+        def live(c):
+            return 0 <= c < ROUNDS
 
         def transpose_x(c):
             x_words = x_tiles[c][:].bitcast(F32)
             x_banks[c] = []
             for b in range(ROUND_TILES[c] // BANK_TILES):
-                xt = psum_x.tile([P, HALVES, BANK_TILES * P], F32)
+                xt = psum_x.tile([P, HALVES, BANK_TILES * P], F32, tag="xt", name="xt")
                 for i in range(BANK_TILES):
                     for u in range(HALVES):
                         nc.tensor.transpose(
@@ -126,9 +139,12 @@ def tile_binaryfactoredlinear_pa_t_kernel(tc, x, U_latent, V_latent, s1, s2, bia
         def quantise_a(c):
             a_mx[c] = quantise(c, a_grouped[c][:].rearrange("p n u e -> p (n u e)"), "a")
 
+        def quantise_h(c):
+            h_mx[c] = quantise(c, h_grouped[c][:].rearrange("m j n s -> m (j n s)"), "h")
+
         def first_matmul(c):
             codes, scales = a_mx[c]
-            h_bf = work.tile([P, ROUND_TILES[c], P, PACK], BF16, align_bytes=64)
+            h_banks[c] = []
             for j in range(ROUND_TILES[c]):
                 tokens = slice(j * P, (j + 1) * P)
                 hT = psum_h.tile([P, PACK, P], F32)
@@ -143,17 +159,44 @@ def tile_binaryfactoredlinear_pa_t_kernel(tc, x, U_latent, V_latent, s1, s2, bia
                         start=True,
                         stop=True,
                     )
-                if c >= ROUNDS - SHARED_ROUNDS and j % 2 == 1:
-                    nc.vector.tensor_copy(out=h_bf[:, j, :, :], in_=hT[:].rearrange("m s n -> m n s"))
-                else:
-                    nc.scalar.copy(out=h_bf[:, j, :, :], in_=hT[:].rearrange("m s n -> m n s"))
-            h_grouped[c] = h_bf
+                h_banks[c].append(hT)
+            h_grouped[c] = work.tile([P, ROUND_TILES[c], P, PACK], BF16, align_bytes=64, name="h_bf")
+
+        def copy_h(c, first, last):
+            for j in range(first, last):
+                nc.scalar.copy(
+                    out=h_grouped[c][:, j, :, :], in_=h_banks[c][j][:].rearrange("m s n -> m n s")
+                )
+
+        def direct(c):
+            return c % 2 == 1 or c == ROUNDS - 1
+
+        def transposed(c):
+            return live(c) and not direct(c)
 
         def second_matmul(c):
             codes, scales = h_mx[c]
-            zT = psum_z.tile([P, ROUND_TILES[c] * P], F32)
+            tiles = ROUND_TILES[c]
+            if c >= ROUNDS - 2:
+                z = psum_x.tile([P, tiles, P], F32, tag="xt", name="z")
+            else:
+                z = psum_z.tile([P, tiles, P], F32, tag="z", name="z")
+            z_banks[c] = z
+            if direct(c):
+                for j in range(tiles):
+                    tokens = slice(j * P, (j + 1) * P)
+                    nc.tensor.matmul_mx(
+                        out=z[:, j, :],
+                        lhsT=codes[:, tokens].bitcast(FP8X4),
+                        lhsT_scale=scales[:, tokens],
+                        rhs=u_codes[:].bitcast(FP8X4),
+                        rhs_scale=u_scales[:],
+                        start=True,
+                        stop=True,
+                    )
+                return
             nc.tensor.matmul_mx(
-                out=zT[:],
+                out=z[:].rearrange("o j n -> o (j n)"),
                 lhsT=u_codes[:].bitcast(FP8X4),
                 lhsT_scale=u_scales[:],
                 rhs=codes[:].bitcast(FP8X4),
@@ -161,30 +204,46 @@ def tile_binaryfactoredlinear_pa_t_kernel(tc, x, U_latent, V_latent, s1, s2, bia
                 start=True,
                 stop=True,
             )
-            oT = work.tile([P, ROUND_TILES[c] * P], F32)
+
+        def scale_zT(c):
+            oT = work.tile([P, ROUND_TILES[c], P], F32)
             nc.scalar.activation(
-                out=oT[:], in_=zT[:], func=ACT.Identity, scale=s1_col[:, 0:1], bias=bias_col[:, 0:1]
+                out=oT[:], in_=z_banks[c][:], func=ACT.Identity, scale=s1_col[:, 0:1], bias=bias_col[:, 0:1]
             )
             outT[c] = oT
 
+        def row(i, c):
+            return s1_bias_rows[:, i, :].unsqueeze(1).to_broadcast([P, ROUND_TILES[c], D_OUT])
+
+        def scale_z(c):
+            product = result_pool.tile([P, ROUND_TILES[c], D_OUT], F32, name="product")
+            nc.vector.tensor_tensor(out=product[:], in0=z_banks[c][:], in1=row(0, c), op=ALU.mult)
+            products[c] = product
+
+        def add_bias(c, engine):
+            result = result_pool.tile([P, ROUND_TILES[c], D_OUT], F32, name="result")
+            engine.tensor_tensor(out=result[:], in0=products[c][:], in1=row(1, c), op=ALU.add)
+            nc.sync.dma_start(out=out_rounds[c], in_=result[:])
+
         def transpose_out(c):
-            o_bank = psum_o.tile([P, ROUND_TILES[c], D_OUT], F32)
+            o_bank = psum_o.tile([P, ROUND_TILES[c], D_OUT], F32, tag="o_bank", name="o_bank")
             for j in range(ROUND_TILES[c]):
-                nc.tensor.transpose(o_bank[:, j, :], outT[c][:, j * P : (j + 1) * P], identity[:])
+                nc.tensor.transpose(o_bank[:, j, :], outT[c][:, j, :], identity[:])
             out_banks[c] = o_bank
 
-        def store_out(c):
-            result = work.tile([P, ROUND_TILES[c], D_OUT], F32)
-            nc.vector.tensor_copy(out=result[:], in_=out_banks[c][:])
+        def store_out(c, copy):
+            result = result_pool.tile([P, ROUND_TILES[c], D_OUT], F32, name="result")
+            copy(out=result[:], in_=out_banks[c][:])
             nc.sync.dma_start(out=out_rounds[c], in_=result[:])
 
         transpose_x(0)
         scale_x(0)
-        quantise_a(0)
         v_grouped = const.tile([P, PACK, P, PACK], BF16, align_bytes=64)
         v_codes = const.tile([P, R], U32, align_bytes=64)
         v_scales = const.tile([P, R], U8, align_bytes=64)
         for s in range(PACK):
+            if s == PACK - 1:
+                quantise_a(0)
             columns = slice(s * P, (s + 1) * P)
             nc.scalar.activation(
                 out=v_grouped[:, s, :, :],
@@ -197,51 +256,74 @@ def tile_binaryfactoredlinear_pa_t_kernel(tc, x, U_latent, V_latent, s1, s2, bia
                 in_=v_grouped[:, s, :, :].rearrange("p m t -> p (m t)"),
             )
 
-        def prepare_u():
-            u_words = u_raw[:].bitcast(F32).rearrange("o (m u) -> o u m", u=HALVES)
-            uT = psum_o.tile([P, HALVES, D_OUT], F32, tag="o_bank")
-            for u in range(HALVES):
-                nc.tensor.transpose(uT[:, u, :], u_words[:, u, :], identity[:])
-            u_grouped = const.tile([P, D_OUT, HALVES, 2], BF16, align_bytes=64)
-            nc.scalar.activation(
-                out=u_grouped[:],
-                in_=uT[:].bitcast(BF16).rearrange("m u (o e) -> m o u e", e=2),
-                func=ACT.Sign,
-            )
-            u_codes = const.tile([P, D_OUT], U32, align_bytes=64)
-            u_scales = const.tile([P, D_OUT], U8, align_bytes=64)
+        transpose_x(1)
+        u_words = u_raw[:].bitcast(F32).rearrange("o (m u) -> o u m", u=HALVES)
+        uT = psum_o.tile([P, HALVES, D_OUT], F32, tag="o_bank")
+        for u in range(HALVES):
+            nc.tensor.transpose(uT[:, u, :], u_words[:, u, :], identity[:])
+        rows_bank = psum_z.tile([P, 2, D_OUT], F32, tag="z", name="rows_bank")
+        nc.tensor.matmul(rows_bank[:], lhsT=ones[:], rhs=rows_bf[:], start=True, stop=True)
+        s1_col = const.tile([P, 1], F32)
+        nc.scalar.activation(out=s1_col[:], in_=s1_bf[:], func=ACT.Identity)
+        bias_col = const.tile([P, 1], F32)
+        nc.scalar.activation(out=bias_col[:], in_=bias_bf[:], func=ACT.Identity)
+        s1_bias_rows = const.tile([P, 2, D_OUT], F32)
+        nc.scalar.copy(out=s1_bias_rows[:], in_=rows_bank[:])
+        u_grouped = const.tile([P, D_OUT, HALVES, 2], BF16, align_bytes=64)
+        nc.scalar.activation(
+            out=u_grouped[:],
+            in_=uT[:].bitcast(BF16).rearrange("m u (o e) -> m o u e", e=2),
+            func=ACT.Sign,
+        )
+        u_codes = const.tile([P, D_OUT], U32, align_bytes=64)
+        u_scales = const.tile([P, D_OUT], U8, align_bytes=64)
+
+        def quantise_u():
             nc.vector.quantize_mx(
                 out=u_codes[:].bitcast(FP8X4),
                 scales=u_scales[:],
                 in_=u_grouped[:].rearrange("m o u e -> m (o u e)"),
             )
-            s1_col = const.tile([P, 1], F32)
-            nc.scalar.activation(out=s1_col[:], in_=s1_bf[:], func=ACT.Identity)
-            bias_col = const.tile([P, 1], F32)
-            nc.scalar.activation(out=bias_col[:], in_=bias_bf[:], func=ACT.Identity)
-            return u_codes, u_scales, s1_col, bias_col
 
-        def live(c):
-            return 0 <= c < ROUNDS
-
-        for n in range(ROUNDS + 3):
-            if live(n + 1):
-                transpose_x(n + 1)
-            if live(n - 3):
-                transpose_out(n - 3)
-            if live(n + 1):
-                scale_x(n + 1)
-            if live(n - 3):
-                store_out(n - 3)
-            if live(n - 1):
-                h_mx[n - 1] = quantise(
-                    n - 1, h_grouped[n - 1][:].rearrange("m j n s -> m (j n s)"), "h"
-                )
-            if live(n + 1):
-                quantise_a(n + 1)
+        scale_x(1)
+        for n in range(ROUNDS):
+            first_matmul(n)
             if live(n - 2):
                 second_matmul(n - 2)
-            if live(n):
-                first_matmul(n)
+            if transposed(n - 3):
+                transpose_out(n - 3)
+            if live(n + 2):
+                transpose_x(n + 2)
+            last = ROUND_TILES[n] - 1
+            copy_h(n, 0, last)
+            if n < ROUNDS - 2:
+                if transposed(n - 2):
+                    scale_zT(n - 2)
+                if transposed(n - 3):
+                    store_out(n - 3, nc.scalar.copy)
+            copy_h(n, last, last + 1)
+            if n == ROUNDS - 1:
+                scale_zT(n - 2)
+            if live(n - 1):
+                quantise_h(n - 1)
+            if live(n + 1):
+                quantise_a(n + 1)
+            if live(n - 2) and direct(n - 2):
+                scale_z(n - 2)
+                add_bias(n - 2, nc.gpsimd)
+            if n == ROUNDS - 2:
+                store_out(n - 3, nc.vector.tensor_copy)
+            if live(n + 2):
+                scale_x(n + 2)
             if n == 0:
-                u_codes, u_scales, s1_col, bias_col = prepare_u()
+                quantise_u()
+
+        second_matmul(ROUNDS - 2)
+        quantise_h(ROUNDS - 1)
+        second_matmul(ROUNDS - 1)
+        transpose_out(ROUNDS - 3)
+        store_out(ROUNDS - 3, nc.scalar.copy)
+        scale_z(ROUNDS - 2)
+        scale_z(ROUNDS - 1)
+        add_bias(ROUNDS - 2, nc.vector)
+        add_bias(ROUNDS - 1, nc.vector)

@@ -96,6 +96,7 @@ def tile_binaryfactoredlinear_pa_t_kernel(tc, x, U_latent, V_latent, s1, s2, bia
         outT = {}
         z_banks = {}
         products = {}
+        results = {}
         out_banks = {}
 
         def live(c):
@@ -179,8 +180,10 @@ def tile_binaryfactoredlinear_pa_t_kernel(tc, x, U_latent, V_latent, s1, s2, bia
             tiles = ROUND_TILES[c]
             if c >= ROUNDS - 2:
                 z = psum_x.tile([P, tiles, P], F32, tag="xt", name="z")
-            else:
+            elif direct(c):
                 z = psum_z.tile([P, tiles, P], F32, tag="z", name="z")
+            else:
+                z = psum_o.tile([P, tiles, P], F32, tag="o_bank", name="z")
             z_banks[c] = z
             if direct(c):
                 for j in range(tiles):
@@ -212,18 +215,27 @@ def tile_binaryfactoredlinear_pa_t_kernel(tc, x, U_latent, V_latent, s1, s2, bia
             )
             outT[c] = oT
 
-        def row(i, c):
-            return s1_bias_rows[:, i, :].unsqueeze(1).to_broadcast([P, ROUND_TILES[c], D_OUT])
+        def row(i, tiles):
+            return s1_bias_rows[:, i, :].unsqueeze(1).to_broadcast([P, tiles, D_OUT])
 
-        def scale_z(c):
-            product = result_pool.tile([P, ROUND_TILES[c], D_OUT], F32, name="product")
-            nc.vector.tensor_tensor(out=product[:], in0=z_banks[c][:], in1=row(0, c), op=ALU.mult)
-            products[c] = product
+        def scale_z(c, first, last):
+            product = result_pool.tile([P, last - first, D_OUT], F32, name="product")
+            nc.vector.tensor_tensor(
+                out=product[:], in0=z_banks[c][:, first:last, :], in1=row(0, last - first), op=ALU.mult
+            )
+            products[c, first] = product
 
-        def add_bias(c, engine):
-            result = result_pool.tile([P, ROUND_TILES[c], D_OUT], F32, name="result")
-            engine.tensor_tensor(out=result[:], in0=products[c][:], in1=row(1, c), op=ALU.add)
-            nc.sync.dma_start(out=out_rounds[c], in_=result[:])
+        def add_bias(c, first, last, engine):
+            if first == 0:
+                results[c] = result_pool.tile([P, ROUND_TILES[c], D_OUT], F32, name="result")
+            engine.tensor_tensor(
+                out=results[c][:, first:last, :],
+                in0=products[c, first][:],
+                in1=row(1, last - first),
+                op=ALU.add,
+            )
+            if last == ROUND_TILES[c]:
+                nc.sync.dma_start(out=out_rounds[c], in_=results[c][:])
 
         def transpose_out(c):
             o_bank = psum_o.tile([P, ROUND_TILES[c], D_OUT], F32, tag="o_bank", name="o_bank")
@@ -309,8 +321,11 @@ def tile_binaryfactoredlinear_pa_t_kernel(tc, x, U_latent, V_latent, s1, s2, bia
             if live(n + 1):
                 quantise_a(n + 1)
             if live(n - 2) and direct(n - 2):
-                scale_z(n - 2)
-                add_bias(n - 2, nc.gpsimd)
+                scale_z(n - 2, 0, 2)
+                add_bias(n - 2, 0, 2, nc.gpsimd)
+            if live(n - 3) and direct(n - 3):
+                scale_z(n - 3, 2, 4)
+                add_bias(n - 3, 2, 4, nc.gpsimd)
             if n == ROUNDS - 2:
                 store_out(n - 3, nc.vector.tensor_copy)
             if live(n + 2):
@@ -323,7 +338,7 @@ def tile_binaryfactoredlinear_pa_t_kernel(tc, x, U_latent, V_latent, s1, s2, bia
         second_matmul(ROUNDS - 1)
         transpose_out(ROUNDS - 3)
         store_out(ROUNDS - 3, nc.scalar.copy)
-        scale_z(ROUNDS - 2)
-        scale_z(ROUNDS - 1)
-        add_bias(ROUNDS - 2, nc.vector)
-        add_bias(ROUNDS - 1, nc.vector)
+        scale_z(ROUNDS - 2, 0, 4)
+        scale_z(ROUNDS - 1, 0, 2)
+        add_bias(ROUNDS - 2, 0, 4, nc.vector)
+        add_bias(ROUNDS - 1, 0, 2, nc.vector)

@@ -131,17 +131,24 @@ def tile_binaryfactoredlinear_pa_t_kernel(tc, x, U_latent, V_latent, s1, s2, bia
                 )
             a_grouped[c] = a_bf
 
-        def quantise(c, grouped_flat, name):
+        def quantise(c, grouped, name, pieces):
             codes = work.tile([P, ROUND_TILES[c] * P], U32, align_bytes=64, name=name + "_codes")
             scales = work.tile([P, ROUND_TILES[c] * P], U8, align_bytes=64, name=name + "_scales")
-            nc.vector.quantize_mx(out=codes[:].bitcast(FP8X4), scales=scales[:], in_=grouped_flat)
+            width = ROUND_TILES[c] * P // pieces
+            for i in range(pieces):
+                words = slice(i * width, (i + 1) * width)
+                nc.vector.quantize_mx(
+                    out=codes[:, words].bitcast(FP8X4),
+                    scales=scales[:, words],
+                    in_=grouped[:, i * width * PACK : (i + 1) * width * PACK],
+                )
             return codes, scales
 
-        def quantise_a(c):
-            a_mx[c] = quantise(c, a_grouped[c][:].rearrange("p n u e -> p (n u e)"), "a")
+        def quantise_a(c, pieces=1):
+            a_mx[c] = quantise(c, a_grouped[c][:].rearrange("p n u e -> p (n u e)"), "a", pieces)
 
         def quantise_h(c):
-            h_mx[c] = quantise(c, h_grouped[c][:].rearrange("m j n s -> m (j n s)"), "h")
+            h_mx[c] = quantise(c, h_grouped[c][:].rearrange("m j n s -> m (j n s)"), "h", 1)
 
         def first_matmul(c):
             codes, scales = a_mx[c]
@@ -249,12 +256,15 @@ def tile_binaryfactoredlinear_pa_t_kernel(tc, x, U_latent, V_latent, s1, s2, bia
             nc.sync.dma_start(out=out_rounds[c], in_=result[:])
 
         transpose_x(0)
-        scale_x(0)
+        rows_bank = psum_z.tile([P, 2, D_OUT], F32, tag="z", name="rows_bank")
+        nc.tensor.matmul(rows_bank[:], lhsT=ones[:], rhs=rows_bf[:], start=True, stop=True)
         v_grouped = const.tile([P, PACK, P, PACK], BF16, align_bytes=64)
         v_codes = const.tile([P, R], U32, align_bytes=64)
         v_scales = const.tile([P, R], U8, align_bytes=64)
         for s in range(PACK):
-            if s == PACK - 1:
+            if s == 2:
+                scale_x(0)
+            if s == 3:
                 quantise_a(0)
             columns = slice(s * P, (s + 1) * P)
             nc.scalar.activation(
@@ -273,8 +283,6 @@ def tile_binaryfactoredlinear_pa_t_kernel(tc, x, U_latent, V_latent, s1, s2, bia
         uT = psum_o.tile([P, HALVES, D_OUT], F32, tag="o_bank")
         for u in range(HALVES):
             nc.tensor.transpose(uT[:, u, :], u_words[:, u, :], identity[:])
-        rows_bank = psum_z.tile([P, 2, D_OUT], F32, tag="z", name="rows_bank")
-        nc.tensor.matmul(rows_bank[:], lhsT=ones[:], rhs=rows_bf[:], start=True, stop=True)
         s1_col = const.tile([P, 1], F32)
         nc.scalar.activation(out=s1_col[:], in_=s1_bf[:], func=ACT.Identity)
         bias_col = const.tile([P, 1], F32)
@@ -316,10 +324,15 @@ def tile_binaryfactoredlinear_pa_t_kernel(tc, x, U_latent, V_latent, s1, s2, bia
             copy_h(n, last, last + 1)
             if n == ROUNDS - 1:
                 scale_zT(n - 2)
-            if live(n - 1):
+            if n == 0:
+                quantise_a(1, 2)
+            elif n == 1:
+                quantise_a(2)
+                quantise_h(0)
+            else:
                 quantise_h(n - 1)
-            if live(n + 1):
-                quantise_a(n + 1)
+                if live(n + 1):
+                    quantise_a(n + 1)
             if live(n - 2) and direct(n - 2):
                 scale_z(n - 2, 0, 2)
                 add_bias(n - 2, 0, 2, nc.gpsimd)
@@ -334,10 +347,10 @@ def tile_binaryfactoredlinear_pa_t_kernel(tc, x, U_latent, V_latent, s1, s2, bia
                 quantise_u()
 
         second_matmul(ROUNDS - 2)
-        quantise_h(ROUNDS - 1)
-        second_matmul(ROUNDS - 1)
         transpose_out(ROUNDS - 3)
         store_out(ROUNDS - 3, nc.scalar.copy)
+        quantise_h(ROUNDS - 1)
+        second_matmul(ROUNDS - 1)
         scale_z(ROUNDS - 2, 0, 4)
         scale_z(ROUNDS - 1, 0, 2)
         add_bias(ROUNDS - 2, 0, 4, nc.vector)

@@ -20,6 +20,7 @@ R = 512
 D_OUT = 128
 ROUND_TILES = [2] + [4] * 15 + [2]
 ROUNDS = len(ROUND_TILES)
+WARM_UPS = 18
 BANK_TILES = 2
 
 FLOPS = 2 * TOKENS * D_IN * R + 2 * TOKENS * R * D_OUT
@@ -49,17 +50,12 @@ def tile_binaryfactoredlinear_pa_t_kernel(tc, x, U_latent, V_latent, s1, s2, bia
         psum_o = ctx.enter_context(tc.psum_pool(name="psum_o", bufs=1))
         ctx.enter_context(tc.manual_schedule())
 
-        s1_bf = const.tile([P, 1], BF16)
-        nc.scalar.dma_start(out=s1_bf[:], in_=s1.rearrange("(o one) -> o one", one=1))
-        bias_bf = const.tile([P, 1], BF16)
-        nc.scalar.dma_start(out=bias_bf[:], in_=bias.rearrange("(o one) -> o one", one=1))
-
-        rows_bf = const.tile([P, 2, D_OUT], BF16)
-        nc.gpsimd.memset(rows_bf[:], 0.0)
+        row_bf = const.tile([P, 2 * D_OUT + D_IN], BF16)
+        nc.vector.memset(row_bf[:].bitcast(U32), 0)
         ones = const.tile([P, P], BF16)
         nc.gpsimd.memset(ones[:], 1.0)
-        nc.scalar.dma_start(out=rows_bf[0:1, 0, :], in_=s1.rearrange("(one o) -> one o", one=1))
-        nc.scalar.dma_start(out=rows_bf[0:1, 1, :], in_=bias.rearrange("(one o) -> one o", one=1))
+        nc.scalar.dma_start(out=row_bf[0:1, :D_OUT], in_=s1.rearrange("(one o) -> one o", one=1))
+        nc.scalar.dma_start(out=row_bf[0:1, D_OUT : 2 * D_OUT], in_=bias.rearrange("(one o) -> one o", one=1))
 
         x_tiles = []
 
@@ -68,16 +64,12 @@ def tile_binaryfactoredlinear_pa_t_kernel(tc, x, U_latent, V_latent, s1, s2, bia
             nc.sync.dma_start(out=x_sb[:], in_=x_rounds[c])
             x_tiles.append(x_sb)
 
-        s2_word = const.tile([P, PACK], BF16)
-        nc.sync.dma_start(
-            out=s2_word[:].rearrange("p (u e) -> p u e", u=HALVES),
-            in_=s2.rearrange("(u p e) -> p u e", u=HALVES, e=2),
-        )
         v_raw = const.tile([P, PACK, R], BF16)
         nc.sync.dma_start(
             out=v_raw[:].rearrange("p (u e) r -> p u (e r)", u=HALVES),
             in_=V_latent.rearrange("(u p e) r -> p u (e r)", u=HALVES, e=2),
         )
+        nc.sync.dma_start(out=row_bf[0:1, 2 * D_OUT :], in_=s2.rearrange("(one k) -> one k", one=1))
         load_x(0)
         load_x(1)
         u_raw = const.tile([P, R], BF16)
@@ -218,12 +210,12 @@ def tile_binaryfactoredlinear_pa_t_kernel(tc, x, U_latent, V_latent, s1, s2, bia
         def scale_zT(c):
             oT = work.tile([P, ROUND_TILES[c], P], F32)
             nc.scalar.activation(
-                out=oT[:], in_=z_banks[c][:], func=ACT.Identity, scale=s1_col[:, 0:1], bias=bias_col[:, 0:1]
+                out=oT[:], in_=z_banks[c][:], func=ACT.Identity, scale=s1_column, bias=bias_column
             )
             outT[c] = oT
 
         def row(i, tiles):
-            return s1_bias_rows[:, i, :].unsqueeze(1).to_broadcast([P, tiles, D_OUT])
+            return s1_bias_rows[:, i * D_OUT : (i + 1) * D_OUT].unsqueeze(1).to_broadcast([P, tiles, D_OUT])
 
         def scale_z(c, first, last):
             product = result_pool.tile([P, last - first, D_OUT], F32, name="product")
@@ -255,9 +247,35 @@ def tile_binaryfactoredlinear_pa_t_kernel(tc, x, U_latent, V_latent, s1, s2, bia
             copy(out=result[:], in_=out_banks[c][:])
             nc.sync.dma_start(out=out_rounds[c], in_=result[:])
 
+        idle_bank = psum_h.tile([P, P], F32, tag="hT", name="idle_bank")
+        for i in range(WARM_UPS):
+            nc.tensor.matmul(idle_bank[:], lhsT=ones[:], rhs=ones[:], start=True, stop=True)
+        s2_bank = psum_z.tile([P, PACK], F32, tag="z", name="s2_bank")
+        for t in range(PACK):
+            u, e = divmod(t, 2)
+            first_k = 2 * D_OUT + 2 * P * u + e
+            nc.tensor.matmul(
+                s2_bank[:, t : t + 1],
+                lhsT=row_bf[:, first_k : first_k + 2 * P - 1 : 2],
+                rhs=ones[:, 0:1],
+                start=True,
+                stop=True,
+            )
+        s2_word = const.tile([P, PACK], BF16)
+        nc.vector.tensor_copy(out=s2_word[:], in_=s2_bank[:])
         transpose_x(0)
-        rows_bank = psum_z.tile([P, 2, D_OUT], F32, tag="z", name="rows_bank")
-        nc.tensor.matmul(rows_bank[:], lhsT=ones[:], rhs=rows_bf[:], start=True, stop=True)
+        rows_columns_bank = psum_o.tile([P, 2 * D_OUT + 2], F32, tag="o_bank", name="rows_columns_bank")
+        nc.tensor.matmul(
+            rows_columns_bank[:, : 2 * D_OUT], lhsT=ones[:], rhs=row_bf[:, : 2 * D_OUT], start=True, stop=True
+        )
+        for i in range(2):
+            nc.tensor.matmul(
+                rows_columns_bank[:, 2 * D_OUT + i : 2 * D_OUT + i + 1],
+                lhsT=row_bf[:, i * D_OUT : (i + 1) * D_OUT],
+                rhs=ones[:, 0:1],
+                start=True,
+                stop=True,
+            )
         v_grouped = const.tile([P, PACK, P, PACK], BF16, align_bytes=64)
         v_codes = const.tile([P, R], U32, align_bytes=64)
         v_scales = const.tile([P, R], U8, align_bytes=64)
@@ -278,17 +296,16 @@ def tile_binaryfactoredlinear_pa_t_kernel(tc, x, U_latent, V_latent, s1, s2, bia
                 in_=v_grouped[:, s, :, :].rearrange("p m t -> p (m t)"),
             )
 
+        s1_bias = const.tile([P, 2 * D_OUT + 2], F32)
+        nc.scalar.copy(out=s1_bias[:], in_=rows_columns_bank[:])
+        s1_bias_rows = s1_bias[:, : 2 * D_OUT]
+        s1_column = s1_bias[:, 2 * D_OUT : 2 * D_OUT + 1]
+        bias_column = s1_bias[:, 2 * D_OUT + 1 :]
         transpose_x(1)
         u_words = u_raw[:].bitcast(F32).rearrange("o (m u) -> o u m", u=HALVES)
-        uT = psum_o.tile([P, HALVES, D_OUT], F32, tag="o_bank")
+        uT = psum_z.tile([P, HALVES, D_OUT], F32, tag="z", name="uT")
         for u in range(HALVES):
             nc.tensor.transpose(uT[:, u, :], u_words[:, u, :], identity[:])
-        s1_col = const.tile([P, 1], F32)
-        nc.scalar.activation(out=s1_col[:], in_=s1_bf[:], func=ACT.Identity)
-        bias_col = const.tile([P, 1], F32)
-        nc.scalar.activation(out=bias_col[:], in_=bias_bf[:], func=ACT.Identity)
-        s1_bias_rows = const.tile([P, 2, D_OUT], F32)
-        nc.scalar.copy(out=s1_bias_rows[:], in_=rows_bank[:])
         u_grouped = const.tile([P, D_OUT, HALVES, 2], BF16, align_bytes=64)
         nc.scalar.activation(
             out=u_grouped[:],

@@ -94,19 +94,19 @@ def tile_binaryfactoredlinear_pa_t_kernel(tc, x, U_latent, V_latent, s1, s2, bia
         def live(c):
             return 0 <= c < ROUNDS
 
-        def transpose_x(c):
+        def transpose_x(c, first):
+            if first >= ROUND_TILES[c]:
+                return
             x_words = x_tiles[c][:].bitcast(F32)
-            x_banks[c] = []
-            for b in range(ROUND_TILES[c] // BANK_TILES):
-                xt = psum_x.tile([P, HALVES, BANK_TILES * P], F32, tag="xt", name="xt")
-                for i in range(BANK_TILES):
-                    for u in range(HALVES):
-                        nc.tensor.transpose(
-                            xt[:, u, i * P : (i + 1) * P],
-                            x_words[:, b * BANK_TILES + i, u * P : (u + 1) * P],
-                            identity[:],
-                        )
-                x_banks[c].append(xt)
+            xt = psum_x.tile([P, HALVES, BANK_TILES * P], F32, tag="xt", name="xt")
+            for i in range(BANK_TILES):
+                for u in range(HALVES):
+                    nc.tensor.transpose(
+                        xt[:, u, i * P : (i + 1) * P],
+                        x_words[:, first + i, u * P : (u + 1) * P],
+                        identity[:],
+                    )
+            x_banks.setdefault(c, []).append(xt)
 
         def scale_x(c):
             a_bf = work.tile([P, ROUND_TILES[c] * P, HALVES, 2], BF16, align_bytes=64)
@@ -162,9 +162,9 @@ def tile_binaryfactoredlinear_pa_t_kernel(tc, x, U_latent, V_latent, s1, s2, bia
                 h_banks[c].append(hT)
             h_grouped[c] = work.tile([P, ROUND_TILES[c], P, PACK], BF16, align_bytes=64, name="h_bf")
 
-        def copy_h(c, first, last):
+        def copy_h(c, first, last, copy):
             for j in range(first, last):
-                nc.scalar.copy(
+                copy(
                     out=h_grouped[c][:, j, :, :], in_=h_banks[c][j][:].rearrange("m s n -> m n s")
                 )
 
@@ -177,7 +177,7 @@ def tile_binaryfactoredlinear_pa_t_kernel(tc, x, U_latent, V_latent, s1, s2, bia
         def second_matmul(c):
             codes, scales = h_mx[c]
             tiles = ROUND_TILES[c]
-            if c >= ROUNDS - 2:
+            if c in (ROUNDS - 3, ROUNDS - 2):
                 z = psum_x.tile([P, tiles, P], F32, tag="xt", name="z")
             elif direct(c):
                 z = psum_z.tile([P, tiles, P], F32, tag="z", name="z")
@@ -237,7 +237,10 @@ def tile_binaryfactoredlinear_pa_t_kernel(tc, x, U_latent, V_latent, s1, s2, bia
                 nc.sync.dma_start(out=out_rounds[c], in_=results[c][:])
 
         def transpose_out(c):
-            o_bank = psum_o.tile([P, ROUND_TILES[c], D_OUT], F32, tag="o_bank", name="o_bank")
+            if c == ROUNDS - 3:
+                o_bank = psum_x.tile([P, ROUND_TILES[c], D_OUT], F32, tag="xt", name="o_bank")
+            else:
+                o_bank = psum_o.tile([P, ROUND_TILES[c], D_OUT], F32, tag="o_bank", name="o_bank")
             for j in range(ROUND_TILES[c]):
                 nc.tensor.transpose(o_bank[:, j, :], outT[c][:, j, :], identity[:])
             out_banks[c] = o_bank
@@ -263,7 +266,7 @@ def tile_binaryfactoredlinear_pa_t_kernel(tc, x, U_latent, V_latent, s1, s2, bia
             )
         s2_word = const.tile([P, PACK], BF16)
         nc.vector.tensor_copy(out=s2_word[:], in_=s2_bank[:])
-        transpose_x(0)
+        transpose_x(0, 0)
         rows_columns_bank = psum_o.tile([P, 2 * D_OUT + 2], F32, tag="o_bank", name="rows_columns_bank")
         nc.tensor.matmul(
             rows_columns_bank[:, : 2 * D_OUT], lhsT=ones[:], rhs=row_bf[:, : 2 * D_OUT], start=True, stop=True
@@ -301,7 +304,8 @@ def tile_binaryfactoredlinear_pa_t_kernel(tc, x, U_latent, V_latent, s1, s2, bia
         s1_bias_rows = s1_bias[:, : 2 * D_OUT]
         s1_column = s1_bias[:, 2 * D_OUT : 2 * D_OUT + 1]
         bias_column = s1_bias[:, 2 * D_OUT + 1 :]
-        transpose_x(1)
+        transpose_x(1, 0)
+        transpose_x(1, 2)
         u_words = u_raw[:].bitcast(F32).rearrange("o (m u) -> o u m", u=HALVES)
         uT = psum_z.tile([P, HALVES, D_OUT], F32, tag="z", name="uT")
         for u in range(HALVES):
@@ -323,24 +327,21 @@ def tile_binaryfactoredlinear_pa_t_kernel(tc, x, U_latent, V_latent, s1, s2, bia
             )
 
         scale_x(1)
-        for n in range(ROUNDS):
+        for n in range(ROUNDS - 2):
             first_matmul(n)
             if live(n - 2):
                 second_matmul(n - 2)
+            transpose_x(n + 2, 0)
             if transposed(n - 3):
                 transpose_out(n - 3)
-            if live(n + 2):
-                transpose_x(n + 2)
+            transpose_x(n + 2, 2)
             last = ROUND_TILES[n] - 1
-            copy_h(n, 0, last)
-            if n < ROUNDS - 2:
-                if transposed(n - 2):
-                    scale_zT(n - 2)
-                if transposed(n - 3):
-                    store_out(n - 3, nc.scalar.copy)
-            copy_h(n, last, last + 1)
-            if n == ROUNDS - 1:
+            copy_h(n, 0, last, nc.scalar.copy)
+            if transposed(n - 2):
                 scale_zT(n - 2)
+            copy_h(n, last, last + 1, nc.scalar.copy)
+            if transposed(n - 3):
+                store_out(n - 3, nc.scalar.copy)
             if n == 0:
                 quantise_a(1, 2)
             elif n == 1:
@@ -348,27 +349,38 @@ def tile_binaryfactoredlinear_pa_t_kernel(tc, x, U_latent, V_latent, s1, s2, bia
                 quantise_h(0)
             else:
                 quantise_h(n - 1)
-                if live(n + 1):
-                    quantise_a(n + 1)
+                quantise_a(n + 1)
             if live(n - 2) and direct(n - 2):
                 scale_z(n - 2, 0, 2)
                 add_bias(n - 2, 0, 2, nc.gpsimd)
             if live(n - 3) and direct(n - 3):
                 scale_z(n - 3, 2, 4)
                 add_bias(n - 3, 2, 4, nc.gpsimd)
-            if n == ROUNDS - 2:
-                store_out(n - 3, nc.vector.tensor_copy)
-            if live(n + 2):
-                scale_x(n + 2)
+            scale_x(n + 2)
             if n == 0:
                 quantise_u()
 
-        second_matmul(ROUNDS - 2)
-        transpose_out(ROUNDS - 3)
-        store_out(ROUNDS - 3, nc.scalar.copy)
+        first_matmul(ROUNDS - 2)
+        copy_h(ROUNDS - 2, 0, 1, nc.vector.tensor_copy)
+        copy_h(ROUNDS - 2, 1, 4, nc.scalar.copy)
+        quantise_a(ROUNDS - 1)
+        first_matmul(ROUNDS - 1)
+        copy_h(ROUNDS - 1, 0, 2, nc.scalar.copy)
+        quantise_h(ROUNDS - 3)
+        second_matmul(ROUNDS - 4)
+        transpose_out(ROUNDS - 5)
+        second_matmul(ROUNDS - 3)
+        scale_zT(ROUNDS - 3)
+        store_out(ROUNDS - 5, nc.scalar.copy)
+        quantise_h(ROUNDS - 2)
+        scale_z(ROUNDS - 4, 0, 4)
         quantise_h(ROUNDS - 1)
+        add_bias(ROUNDS - 4, 0, 4, nc.gpsimd)
+        second_matmul(ROUNDS - 2)
         second_matmul(ROUNDS - 1)
+        transpose_out(ROUNDS - 3)
         scale_z(ROUNDS - 2, 0, 4)
         scale_z(ROUNDS - 1, 0, 2)
         add_bias(ROUNDS - 2, 0, 4, nc.vector)
+        store_out(ROUNDS - 3, nc.scalar.copy)
         add_bias(ROUNDS - 1, 0, 2, nc.vector)

@@ -142,10 +142,9 @@ def tile_binaryfactoredlinear_pa_t_kernel(tc, x, U_latent, V_latent, s1, s2, bia
         def quantise_h(c):
             h_mx[c] = quantise(c, h_grouped[c][:].rearrange("m j n s -> m (j n s)"), "h", 1)
 
-        def first_matmul(c):
+        def first_matmul(c, first, last):
             codes, scales = a_mx[c]
-            h_banks[c] = []
-            for j in range(ROUND_TILES[c]):
+            for j in range(first, last):
                 tokens = slice(j * P, (j + 1) * P)
                 hT = psum_h.tile([P, PACK, P], F32)
                 for s in range(PACK):
@@ -159,7 +158,9 @@ def tile_binaryfactoredlinear_pa_t_kernel(tc, x, U_latent, V_latent, s1, s2, bia
                         start=True,
                         stop=True,
                     )
-                h_banks[c].append(hT)
+                h_banks.setdefault(c, []).append(hT)
+
+        def new_h(c):
             h_grouped[c] = work.tile([P, ROUND_TILES[c], P, PACK], BF16, align_bytes=64, name="h_bf")
 
         def copy_h(c, first, last, copy):
@@ -328,14 +329,18 @@ def tile_binaryfactoredlinear_pa_t_kernel(tc, x, U_latent, V_latent, s1, s2, bia
 
         scale_x(1)
         for n in range(ROUNDS - 2):
-            first_matmul(n)
-            if live(n - 2):
+            last = ROUND_TILES[n] - 1
+            new_h(n)
+            first_matmul(n, 0, last)
+            if live(n - 2) and direct(n - 2):
+                second_matmul(n - 2)
+            first_matmul(n, last, last + 1)
+            if transposed(n - 2):
                 second_matmul(n - 2)
             transpose_x(n + 2, 0)
             if transposed(n - 3):
                 transpose_out(n - 3)
             transpose_x(n + 2, 2)
-            last = ROUND_TILES[n] - 1
             copy_h(n, 0, last, nc.scalar.copy)
             if transposed(n - 2):
                 scale_zT(n - 2)
@@ -360,11 +365,13 @@ def tile_binaryfactoredlinear_pa_t_kernel(tc, x, U_latent, V_latent, s1, s2, bia
             if n == 0:
                 quantise_u()
 
-        first_matmul(ROUNDS - 2)
+        new_h(ROUNDS - 2)
+        first_matmul(ROUNDS - 2, 0, 4)
         copy_h(ROUNDS - 2, 0, 1, nc.vector.tensor_copy)
         copy_h(ROUNDS - 2, 1, 4, nc.scalar.copy)
         quantise_a(ROUNDS - 1)
-        first_matmul(ROUNDS - 1)
+        new_h(ROUNDS - 1)
+        first_matmul(ROUNDS - 1, 0, 2)
         copy_h(ROUNDS - 1, 0, 2, nc.scalar.copy)
         quantise_h(ROUNDS - 3)
         second_matmul(ROUNDS - 4)
@@ -377,10 +384,10 @@ def tile_binaryfactoredlinear_pa_t_kernel(tc, x, U_latent, V_latent, s1, s2, bia
         quantise_h(ROUNDS - 1)
         add_bias(ROUNDS - 4, 0, 4, nc.gpsimd)
         second_matmul(ROUNDS - 2)
-        second_matmul(ROUNDS - 1)
         transpose_out(ROUNDS - 3)
-        scale_z(ROUNDS - 2, 0, 4)
-        scale_z(ROUNDS - 1, 0, 2)
-        add_bias(ROUNDS - 2, 0, 4, nc.vector)
         store_out(ROUNDS - 3, nc.scalar.copy)
+        second_matmul(ROUNDS - 1)
+        scale_z(ROUNDS - 2, 0, 4)
+        add_bias(ROUNDS - 2, 0, 4, nc.vector)
+        scale_z(ROUNDS - 1, 0, 2)
         add_bias(ROUNDS - 1, 0, 2, nc.vector)

@@ -290,8 +290,8 @@ def tile_binaryfactoredlinear_pa_t_kernel(tc, x, U_latent, V_latent, s1, s2, bia
                 quantise_a(0)
             columns = slice(s * P, (s + 1) * P)
             nc.scalar.activation(
-                out=v_grouped[:, s, :, :],
-                in_=v_raw[:].rearrange("p t (m s) -> p s m t", s=PACK)[:, s, :, :],
+                out=v_grouped[:, s, :, :].rearrange("p (c i) t -> p c t i", i=PACK),
+                in_=v_raw[:].rearrange("p t (c i s) -> p s c t i", i=PACK, s=PACK)[:, s, :, :, :],
                 func=ACT.Sign,
             )
             nc.vector.quantize_mx(

@@ -59,19 +59,22 @@ def tile_binaryfactoredlinear_pa_t_kernel(tc, x, U_latent, V_latent, s1, s2, bia
 
         x_tiles = []
 
-        def load_x(c):
+        def load_x(c, pieces=1):
             x_sb = x_pool.tile([P, ROUND_TILES[c], D_IN], BF16)
-            nc.sync.dma_start(out=x_sb[:], in_=x_rounds[c])
+            width = ROUND_TILES[c] // pieces
+            for i in range(pieces):
+                tiles = slice(i * width, (i + 1) * width)
+                nc.sync.dma_start(out=x_sb[:, tiles, :], in_=x_rounds[c][:, tiles, :])
             x_tiles.append(x_sb)
 
+        load_x(0)
+        nc.sync.dma_start(out=row_bf[0:1, 2 * D_OUT :], in_=s2.rearrange("(one k) -> one k", one=1))
         v_raw = const.tile([P, PACK, R], BF16)
         nc.sync.dma_start(
             out=v_raw[:].rearrange("p (u e) r -> p u (e r)", u=HALVES),
             in_=V_latent.rearrange("(u p e) r -> p u (e r)", u=HALVES, e=2),
         )
-        nc.sync.dma_start(out=row_bf[0:1, 2 * D_OUT :], in_=s2.rearrange("(one k) -> one k", one=1))
-        load_x(0)
-        load_x(1)
+        load_x(1, 2)
         u_raw = const.tile([P, R], BF16)
         nc.sync.dma_start(out=u_raw[:], in_=U_latent)
         for c in range(2, ROUNDS):
@@ -108,12 +111,16 @@ def tile_binaryfactoredlinear_pa_t_kernel(tc, x, U_latent, V_latent, s1, s2, bia
                     )
             x_banks.setdefault(c, []).append(xt)
 
-        def scale_x(c):
-            a_bf = work.tile([P, ROUND_TILES[c] * P, HALVES, 2], BF16, align_bytes=64)
+        def scale_x(c, first, last):
+            if first == 0:
+                a_grouped[c] = work.tile(
+                    [P, ROUND_TILES[c] * P, HALVES, 2], BF16, align_bytes=64, name="a_bf"
+                )
             bank_tokens = BANK_TILES * P
-            for b, xt in enumerate(x_banks[c]):
+            for b in range(first, last):
+                xt = x_banks[c][b]
                 nc.vector.tensor_tensor(
-                    out=a_bf[:, b * bank_tokens : (b + 1) * bank_tokens, :, :],
+                    out=a_grouped[c][:, b * bank_tokens : (b + 1) * bank_tokens, :, :],
                     in0=xt[:].bitcast(BF16).rearrange("p u (n e) -> p n u e", e=2),
                     in1=s2_word[:]
                     .rearrange("p (u e) -> p u e", u=HALVES)
@@ -121,7 +128,6 @@ def tile_binaryfactoredlinear_pa_t_kernel(tc, x, U_latent, V_latent, s1, s2, bia
                     .to_broadcast([P, bank_tokens, HALVES, 2]),
                     op=ALU.mult,
                 )
-            a_grouped[c] = a_bf
 
         def quantise(c, grouped, name, pieces):
             codes = work.tile([P, ROUND_TILES[c] * P], U32, align_bytes=64, name=name + "_codes")
@@ -180,6 +186,8 @@ def tile_binaryfactoredlinear_pa_t_kernel(tc, x, U_latent, V_latent, s1, s2, bia
             tiles = ROUND_TILES[c]
             if c in (ROUNDS - 3, ROUNDS - 2):
                 z = psum_x.tile([P, tiles, P], F32, tag="xt", name="z")
+            elif c == ROUNDS - 1:
+                z = psum_h.tile([P, tiles, P], F32, tag="hT", name="z")
             elif direct(c):
                 z = psum_z.tile([P, tiles, P], F32, tag="z", name="z")
             else:
@@ -234,7 +242,9 @@ def tile_binaryfactoredlinear_pa_t_kernel(tc, x, U_latent, V_latent, s1, s2, bia
                 in1=row(1, last - first),
                 op=ALU.add,
             )
-            if last == ROUND_TILES[c]:
+            if c == ROUNDS - 2:
+                nc.sync.dma_start(out=out_rounds[c][:, first:last, :], in_=results[c][:, first:last, :])
+            elif last == ROUND_TILES[c]:
                 nc.sync.dma_start(out=out_rounds[c], in_=results[c][:])
 
         def transpose_out(c):
@@ -246,10 +256,11 @@ def tile_binaryfactoredlinear_pa_t_kernel(tc, x, U_latent, V_latent, s1, s2, bia
                 nc.tensor.transpose(o_bank[:, j, :], outT[c][:, j, :], identity[:])
             out_banks[c] = o_bank
 
-        def store_out(c, copy):
+        def store_out(c):
             result = result_pool.tile([P, ROUND_TILES[c], D_OUT], F32, name="result")
-            copy(out=result[:], in_=out_banks[c][:])
-            nc.sync.dma_start(out=out_rounds[c], in_=result[:])
+            nc.scalar.copy(out=result[:], in_=out_banks[c][:])
+            queue = nc.scalar if c == ROUNDS - 3 else nc.sync
+            queue.dma_start(out=out_rounds[c], in_=result[:])
 
         idle_bank = psum_h.tile([P, P], F32, tag="hT", name="idle_bank")
         for i in range(WARM_UPS):
@@ -283,11 +294,14 @@ def tile_binaryfactoredlinear_pa_t_kernel(tc, x, U_latent, V_latent, s1, s2, bia
         v_grouped = const.tile([P, PACK, P, PACK], BF16, align_bytes=64)
         v_codes = const.tile([P, R], U32, align_bytes=64)
         v_scales = const.tile([P, R], U8, align_bytes=64)
+        scale_x(0, 0, 1)
         for s in range(PACK):
-            if s == 2:
-                scale_x(0)
-            if s == 3:
+            if s == 0:
                 quantise_a(0)
+            if s == 2:
+                transpose_x(1, 0)
+                transpose_x(1, 2)
+                scale_x(1, 0, 1)
             columns = slice(s * P, (s + 1) * P)
             nc.scalar.activation(
                 out=v_grouped[:, s, :, :].rearrange("p (c i) t -> p c t i", i=PACK),
@@ -305,8 +319,6 @@ def tile_binaryfactoredlinear_pa_t_kernel(tc, x, U_latent, V_latent, s1, s2, bia
         s1_bias_rows = s1_bias[:, : 2 * D_OUT]
         s1_column = s1_bias[:, 2 * D_OUT : 2 * D_OUT + 1]
         bias_column = s1_bias[:, 2 * D_OUT + 1 :]
-        transpose_x(1, 0)
-        transpose_x(1, 2)
         u_words = u_raw[:].bitcast(F32).rearrange("o (m u) -> o u m", u=HALVES)
         uT = psum_z.tile([P, HALVES, D_OUT], F32, tag="z", name="uT")
         for u in range(HALVES):
@@ -327,7 +339,7 @@ def tile_binaryfactoredlinear_pa_t_kernel(tc, x, U_latent, V_latent, s1, s2, bia
                 in_=u_grouped[:].rearrange("m o u e -> m (o u e)"),
             )
 
-        scale_x(1)
+        scale_x(1, 1, 2)
         for n in range(ROUNDS - 2):
             last = ROUND_TILES[n] - 1
             new_h(n)
@@ -346,7 +358,7 @@ def tile_binaryfactoredlinear_pa_t_kernel(tc, x, U_latent, V_latent, s1, s2, bia
                 scale_zT(n - 2)
             copy_h(n, last, last + 1, nc.scalar.copy)
             if transposed(n - 3):
-                store_out(n - 3, nc.scalar.copy)
+                store_out(n - 3)
             if n == 0:
                 quantise_a(1, 2)
             elif n == 1:
@@ -361,12 +373,15 @@ def tile_binaryfactoredlinear_pa_t_kernel(tc, x, U_latent, V_latent, s1, s2, bia
             if live(n - 3) and direct(n - 3):
                 scale_z(n - 3, 2, 4)
                 add_bias(n - 3, 2, 4, nc.gpsimd)
-            scale_x(n + 2)
+            scale_x(n + 2, 0, len(x_banks[n + 2]))
             if n == 0:
                 quantise_u()
 
         new_h(ROUNDS - 2)
-        first_matmul(ROUNDS - 2, 0, 4)
+        first_matmul(ROUNDS - 2, 0, 3)
+        second_matmul(ROUNDS - 4)
+        first_matmul(ROUNDS - 2, 3, 4)
+        transpose_out(ROUNDS - 5)
         copy_h(ROUNDS - 2, 0, 1, nc.vector.tensor_copy)
         copy_h(ROUNDS - 2, 1, 4, nc.scalar.copy)
         quantise_a(ROUNDS - 1)
@@ -374,20 +389,20 @@ def tile_binaryfactoredlinear_pa_t_kernel(tc, x, U_latent, V_latent, s1, s2, bia
         first_matmul(ROUNDS - 1, 0, 2)
         copy_h(ROUNDS - 1, 0, 2, nc.scalar.copy)
         quantise_h(ROUNDS - 3)
-        second_matmul(ROUNDS - 4)
-        transpose_out(ROUNDS - 5)
-        second_matmul(ROUNDS - 3)
-        scale_zT(ROUNDS - 3)
-        store_out(ROUNDS - 5, nc.scalar.copy)
-        quantise_h(ROUNDS - 2)
         scale_z(ROUNDS - 4, 0, 4)
+        second_matmul(ROUNDS - 3)
+        store_out(ROUNDS - 5)
+        scale_zT(ROUNDS - 3)
+        quantise_h(ROUNDS - 2)
+        add_bias(ROUNDS - 4, 0, 4, nc.vector)
         quantise_h(ROUNDS - 1)
-        add_bias(ROUNDS - 4, 0, 4, nc.gpsimd)
         second_matmul(ROUNDS - 2)
-        transpose_out(ROUNDS - 3)
-        store_out(ROUNDS - 3, nc.scalar.copy)
         second_matmul(ROUNDS - 1)
-        scale_z(ROUNDS - 2, 0, 4)
-        add_bias(ROUNDS - 2, 0, 4, nc.vector)
+        transpose_out(ROUNDS - 3)
+        store_out(ROUNDS - 3)
+        scale_z(ROUNDS - 2, 0, 2)
+        scale_z(ROUNDS - 2, 2, 4)
+        add_bias(ROUNDS - 2, 0, 2, nc.vector)
         scale_z(ROUNDS - 1, 0, 2)
+        add_bias(ROUNDS - 2, 2, 4, nc.vector)
         add_bias(ROUNDS - 1, 0, 2, nc.vector)

@@ -59,22 +59,19 @@ def tile_binaryfactoredlinear_pa_t_kernel(tc, x, U_latent, V_latent, s1, s2, bia
 
         x_tiles = []
 
-        def load_x(c, pieces=1):
+        def load_x(c):
             x_sb = x_pool.tile([P, ROUND_TILES[c], D_IN], BF16)
-            width = ROUND_TILES[c] // pieces
-            for i in range(pieces):
-                tiles = slice(i * width, (i + 1) * width)
-                nc.sync.dma_start(out=x_sb[:, tiles, :], in_=x_rounds[c][:, tiles, :])
+            nc.sync.dma_start(out=x_sb[:], in_=x_rounds[c])
             x_tiles.append(x_sb)
 
-        load_x(0)
-        nc.sync.dma_start(out=row_bf[0:1, 2 * D_OUT :], in_=s2.rearrange("(one k) -> one k", one=1))
         v_raw = const.tile([P, PACK, R], BF16)
         nc.sync.dma_start(
             out=v_raw[:].rearrange("p (u e) r -> p u (e r)", u=HALVES),
             in_=V_latent.rearrange("(u p e) r -> p u (e r)", u=HALVES, e=2),
         )
-        load_x(1, 2)
+        nc.sync.dma_start(out=row_bf[0:1, 2 * D_OUT :], in_=s2.rearrange("(one k) -> one k", one=1))
+        load_x(0)
+        load_x(1)
         u_raw = const.tile([P, R], BF16)
         nc.sync.dma_start(out=u_raw[:], in_=U_latent)
         for c in range(2, ROUNDS):
@@ -111,16 +108,12 @@ def tile_binaryfactoredlinear_pa_t_kernel(tc, x, U_latent, V_latent, s1, s2, bia
                     )
             x_banks.setdefault(c, []).append(xt)
 
-        def scale_x(c, first, last):
-            if first == 0:
-                a_grouped[c] = work.tile(
-                    [P, ROUND_TILES[c] * P, HALVES, 2], BF16, align_bytes=64, name="a_bf"
-                )
+        def scale_x(c):
+            a_bf = work.tile([P, ROUND_TILES[c] * P, HALVES, 2], BF16, align_bytes=64)
             bank_tokens = BANK_TILES * P
-            for b in range(first, last):
-                xt = x_banks[c][b]
+            for b, xt in enumerate(x_banks[c]):
                 nc.vector.tensor_tensor(
-                    out=a_grouped[c][:, b * bank_tokens : (b + 1) * bank_tokens, :, :],
+                    out=a_bf[:, b * bank_tokens : (b + 1) * bank_tokens, :, :],
                     in0=xt[:].bitcast(BF16).rearrange("p u (n e) -> p n u e", e=2),
                     in1=s2_word[:]
                     .rearrange("p (u e) -> p u e", u=HALVES)
@@ -128,6 +121,7 @@ def tile_binaryfactoredlinear_pa_t_kernel(tc, x, U_latent, V_latent, s1, s2, bia
                     .to_broadcast([P, bank_tokens, HALVES, 2]),
                     op=ALU.mult,
                 )
+            a_grouped[c] = a_bf
 
         def quantise(c, grouped, name, pieces):
             codes = work.tile([P, ROUND_TILES[c] * P], U32, align_bytes=64, name=name + "_codes")
@@ -294,14 +288,11 @@ def tile_binaryfactoredlinear_pa_t_kernel(tc, x, U_latent, V_latent, s1, s2, bia
         v_grouped = const.tile([P, PACK, P, PACK], BF16, align_bytes=64)
         v_codes = const.tile([P, R], U32, align_bytes=64)
         v_scales = const.tile([P, R], U8, align_bytes=64)
-        scale_x(0, 0, 1)
         for s in range(PACK):
-            if s == 0:
-                quantise_a(0)
             if s == 2:
-                transpose_x(1, 0)
-                transpose_x(1, 2)
-                scale_x(1, 0, 1)
+                scale_x(0)
+            if s == 3:
+                quantise_a(0)
             columns = slice(s * P, (s + 1) * P)
             nc.scalar.activation(
                 out=v_grouped[:, s, :, :].rearrange("p (c i) t -> p c t i", i=PACK),
@@ -319,6 +310,8 @@ def tile_binaryfactoredlinear_pa_t_kernel(tc, x, U_latent, V_latent, s1, s2, bia
         s1_bias_rows = s1_bias[:, : 2 * D_OUT]
         s1_column = s1_bias[:, 2 * D_OUT : 2 * D_OUT + 1]
         bias_column = s1_bias[:, 2 * D_OUT + 1 :]
+        transpose_x(1, 0)
+        transpose_x(1, 2)
         u_words = u_raw[:].bitcast(F32).rearrange("o (m u) -> o u m", u=HALVES)
         uT = psum_z.tile([P, HALVES, D_OUT], F32, tag="z", name="uT")
         for u in range(HALVES):
@@ -339,7 +332,7 @@ def tile_binaryfactoredlinear_pa_t_kernel(tc, x, U_latent, V_latent, s1, s2, bia
                 in_=u_grouped[:].rearrange("m o u e -> m (o u e)"),
             )
 
-        scale_x(1, 1, 2)
+        scale_x(1)
         for n in range(ROUNDS - 2):
             last = ROUND_TILES[n] - 1
             new_h(n)
@@ -373,7 +366,7 @@ def tile_binaryfactoredlinear_pa_t_kernel(tc, x, U_latent, V_latent, s1, s2, bia
             if live(n - 3) and direct(n - 3):
                 scale_z(n - 3, 2, 4)
                 add_bias(n - 3, 2, 4, nc.gpsimd)
-            scale_x(n + 2, 0, len(x_banks[n + 2]))
+            scale_x(n + 2)
             if n == 0:
                 quantise_u()
 

@@ -20,7 +20,7 @@ R = 512
 D_OUT = 128
 ROUND_TILES = [2] + [4] * 15 + [2]
 ROUNDS = len(ROUND_TILES)
-WARM_UPS = 18
+WARM_UPS = (24, 6, 4)
 BANK_TILES = 2
 
 FLOPS = 2 * TOKENS * D_IN * R + 2 * TOKENS * R * D_OUT
@@ -257,8 +257,12 @@ def tile_binaryfactoredlinear_pa_t_kernel(tc, x, U_latent, V_latent, s1, s2, bia
             queue.dma_start(out=out_rounds[c], in_=result[:])
 
         idle_bank = psum_h.tile([P, P], F32, tag="hT", name="idle_bank")
-        for i in range(WARM_UPS):
-            nc.tensor.matmul(idle_bank[:], lhsT=ones[:], rhs=ones[:], start=True, stop=True)
+
+        def warm_up(count):
+            for i in range(count):
+                nc.tensor.matmul(idle_bank[:], lhsT=ones[:], rhs=ones[:], start=True, stop=True)
+
+        warm_up(WARM_UPS[0])
         s2_bank = psum_z.tile([P, PACK], F32, tag="z", name="s2_bank")
         for t in range(PACK):
             u, e = divmod(t, 2)
@@ -285,6 +289,7 @@ def tile_binaryfactoredlinear_pa_t_kernel(tc, x, U_latent, V_latent, s1, s2, bia
                 start=True,
                 stop=True,
             )
+        warm_up(WARM_UPS[1])
         v_grouped = const.tile([P, PACK, P, PACK], BF16, align_bytes=64)
         v_codes = const.tile([P, R], U32, align_bytes=64)
         v_scales = const.tile([P, R], U8, align_bytes=64)
@@ -316,6 +321,7 @@ def tile_binaryfactoredlinear_pa_t_kernel(tc, x, U_latent, V_latent, s1, s2, bia
         uT = psum_z.tile([P, HALVES, D_OUT], F32, tag="z", name="uT")
         for u in range(HALVES):
             nc.tensor.transpose(uT[:, u, :], u_words[:, u, :], identity[:])
+        warm_up(WARM_UPS[2])
         u_grouped = const.tile([P, D_OUT, HALVES, 2], BF16, align_bytes=64)
         nc.scalar.activation(
             out=u_grouped[:],

from contextlib import ExitStack

import concourse.mybir as mybir
from concourse.masks import make_identity

BF16 = mybir.dt.bfloat16
F32 = mybir.dt.float32
U32 = mybir.dt.uint32
U8 = mybir.dt.uint8
FP8X4 = mybir.dt.float8_e4m3fn_x4
ALU = mybir.AluOpType
ACT = mybir.ActivationFunctionType

P = 128
PACK = 4
HALVES = 2
TOKENS = 4 * 2048
D_IN = 512
R = 512
D_OUT = 128
ROUND_TILES = [2] + [4] * 15 + [2]
ROUNDS = len(ROUND_TILES)
WARM_UPS = (24, 6, 4)
BANK_TILES = 2

FLOPS = 2 * TOKENS * D_IN * R + 2 * TOKENS * R * D_OUT


def tile_binaryfactoredlinear_pa_t_kernel(tc, x, U_latent, V_latent, s1, s2, bias, out):
    nc = tc.nc
    x_tokens = x.flatten_outer_dims()
    out_tokens = out.flatten_outer_dims()
    x_rounds = []
    out_rounds = []
    first_token = 0
    for tiles in ROUND_TILES:
        rows = slice(first_token, first_token + tiles * P)
        x_rounds.append(x_tokens[rows, :].rearrange("(p j) k -> p j k", j=tiles))
        out_rounds.append(out_tokens[rows, :].rearrange("(p j) o -> p j o", j=tiles))
        first_token += tiles * P

    with ExitStack() as ctx:
        const = ctx.enter_context(tc.tile_pool(name="const", bufs=1))
        x_pool = ctx.enter_context(tc.tile_pool(name="x_pool", bufs=ROUNDS))
        result_pool = ctx.enter_context(tc.tile_pool(name="result_pool", bufs=8))
        work = ctx.enter_context(tc.tile_pool(name="work", bufs=3))
        psum_x = ctx.enter_context(tc.psum_pool(name="psum_x", bufs=2))
        psum_h = ctx.enter_context(tc.psum_pool(name="psum_h", bufs=4))
        psum_z = ctx.enter_context(tc.psum_pool(name="psum_z", bufs=1))
        psum_o = ctx.enter_context(tc.psum_pool(name="psum_o", bufs=1))
        ctx.enter_context(tc.manual_schedule())

        row_bf = const.tile([P, 2 * D_OUT + D_IN], BF16)
        nc.vector.memset(row_bf[:].bitcast(U32), 0)
        ones = const.tile([P, P], BF16)
        nc.gpsimd.memset(ones[:], 1.0)
        nc.scalar.dma_start(out=row_bf[0:1, :D_OUT], in_=s1.rearrange("(one o) -> one o", one=1))
        nc.scalar.dma_start(out=row_bf[0:1, D_OUT : 2 * D_OUT], in_=bias.rearrange("(one o) -> one o", one=1))

        x_tiles = []

        def load_x(c):
            x_sb = x_pool.tile([P, ROUND_TILES[c], D_IN], BF16)
            nc.sync.dma_start(out=x_sb[:], in_=x_rounds[c])
            x_tiles.append(x_sb)

        v_raw = const.tile([P, PACK, R], BF16)
        nc.sync.dma_start(
            out=v_raw[:].rearrange("p (u e) r -> p u (e r)", u=HALVES),
            in_=V_latent.rearrange("(u p e) r -> p u (e r)", u=HALVES, e=2),
        )
        nc.sync.dma_start(out=row_bf[0:1, 2 * D_OUT :], in_=s2.rearrange("(one k) -> one k", one=1))
        load_x(0)
        load_x(1)
        u_raw = const.tile([P, R], BF16)
        nc.sync.dma_start(out=u_raw[:], in_=U_latent)
        for c in range(2, ROUNDS):
            load_x(c)
        identity = const.tile([P, P], F32)
        make_identity(nc, identity[:])

        x_banks = {}
        a_grouped = {}
        a_mx = {}
        h_banks = {}
        h_grouped = {}
        h_mx = {}
        outT = {}
        z_banks = {}
        products = {}
        results = {}
        out_banks = {}

        def live(c):
            return 0 <= c < ROUNDS

        def transpose_x(c, first):
            if first >= ROUND_TILES[c]:
                return
            x_words = x_tiles[c][:].bitcast(F32)
            xt = psum_x.tile([P, HALVES, BANK_TILES * P], F32, tag="xt", name="xt")
            for i in range(BANK_TILES):
                for u in range(HALVES):
                    nc.tensor.transpose(
                        xt[:, u, i * P : (i + 1) * P],
                        x_words[:, first + i, u * P : (u + 1) * P],
                        identity[:],
                    )
            x_banks.setdefault(c, []).append(xt)

        def scale_x(c):
            a_bf = work.tile([P, ROUND_TILES[c] * P, HALVES, 2], BF16, align_bytes=64)
            bank_tokens = BANK_TILES * P
            for b, xt in enumerate(x_banks[c]):
                nc.vector.tensor_tensor(
                    out=a_bf[:, b * bank_tokens : (b + 1) * bank_tokens, :, :],
                    in0=xt[:].bitcast(BF16).rearrange("p u (n e) -> p n u e", e=2),
                    in1=s2_word[:]
                    .rearrange("p (u e) -> p u e", u=HALVES)
                    .unsqueeze(1)
                    .to_broadcast([P, bank_tokens, HALVES, 2]),
                    op=ALU.mult,
                )
            a_grouped[c] = a_bf

        def quantise(c, grouped, name, pieces):
            codes = work.tile([P, ROUND_TILES[c] * P], U32, align_bytes=64, name=name + "_codes")
            scales = work.tile([P, ROUND_TILES[c] * P], U8, align_bytes=64, name=name + "_scales")
            width = ROUND_TILES[c] * P // pieces
            for i in range(pieces):
                words = slice(i * width, (i + 1) * width)
                nc.vector.quantize_mx(
                    out=codes[:, words].bitcast(FP8X4),
                    scales=scales[:, words],
                    in_=grouped[:, i * width * PACK : (i + 1) * width * PACK],
                )
            return codes, scales

        def quantise_a(c, pieces=1):
            a_mx[c] = quantise(c, a_grouped[c][:].rearrange("p n u e -> p (n u e)"), "a", pieces)

        def quantise_h(c):
            h_mx[c] = quantise(c, h_grouped[c][:].rearrange("m j n s -> m (j n s)"), "h", 1)

        def first_matmul(c, first, last):
            codes, scales = a_mx[c]
            for j in range(first, last):
                tokens = slice(j * P, (j + 1) * P)
                hT = psum_h.tile([P, PACK, P], F32)
                for s in range(PACK):
                    columns = slice(s * P, (s + 1) * P)
                    nc.tensor.matmul_mx(
                        out=hT[:, s, :],
                        lhsT=v_codes[:, columns].bitcast(FP8X4),
                        lhsT_scale=v_scales[:, columns],
                        rhs=codes[:, tokens].bitcast(FP8X4),
                        rhs_scale=scales[:, tokens],
                        start=True,
                        stop=True,
                    )
                h_banks.setdefault(c, []).append(hT)

        def new_h(c):
            h_grouped[c] = work.tile([P, ROUND_TILES[c], P, PACK], BF16, align_bytes=64, name="h_bf")

        def copy_h(c, first, last, copy):
            for j in range(first, last):
                copy(
                    out=h_grouped[c][:, j, :, :], in_=h_banks[c][j][:].rearrange("m s n -> m n s")
                )

        def direct(c):
            return c % 2 == 1 or c == ROUNDS - 1

        def transposed(c):
            return live(c) and not direct(c)

        def second_matmul(c):
            codes, scales = h_mx[c]
            tiles = ROUND_TILES[c]
            if c in (ROUNDS - 3, ROUNDS - 2):
                z = psum_x.tile([P, tiles, P], F32, tag="xt", name="z")
            elif c == ROUNDS - 1:
                z = psum_h.tile([P, tiles, P], F32, tag="hT", name="z")
            elif direct(c):
                z = psum_z.tile([P, tiles, P], F32, tag="z", name="z")
            else:
                z = psum_o.tile([P, tiles, P], F32, tag="o_bank", name="z")
            z_banks[c] = z
            if direct(c):
                for j in range(tiles):
                    tokens = slice(j * P, (j + 1) * P)
                    nc.tensor.matmul_mx(
                        out=z[:, j, :],
                        lhsT=codes[:, tokens].bitcast(FP8X4),
                        lhsT_scale=scales[:, tokens],
                        rhs=u_codes[:].bitcast(FP8X4),
                        rhs_scale=u_scales[:],
                        start=True,
                        stop=True,
                    )
                return
            nc.tensor.matmul_mx(
                out=z[:].rearrange("o j n -> o (j n)"),
                lhsT=u_codes[:].bitcast(FP8X4),
                lhsT_scale=u_scales[:],
                rhs=codes[:].bitcast(FP8X4),
                rhs_scale=scales[:],
                start=True,
                stop=True,
            )

        def scale_zT(c):
            oT = work.tile([P, ROUND_TILES[c], P], F32)
            nc.scalar.activation(
                out=oT[:], in_=z_banks[c][:], func=ACT.Identity, scale=s1_column, bias=bias_column
            )
            outT[c] = oT

        def row(i, tiles):
            return s1_bias_rows[:, i * D_OUT : (i + 1) * D_OUT].unsqueeze(1).to_broadcast([P, tiles, D_OUT])

        def scale_z(c, first, last):
            product = result_pool.tile([P, last - first, D_OUT], F32, name="product")
            nc.vector.tensor_tensor(
                out=product[:], in0=z_banks[c][:, first:last, :], in1=row(0, last - first), op=ALU.mult
            )
            products[c, first] = product

        def add_bias(c, first, last, engine):
            if first == 0:
                results[c] = result_pool.tile([P, ROUND_TILES[c], D_OUT], F32, name="result")
            engine.tensor_tensor(
                out=results[c][:, first:last, :],
                in0=products[c, first][:],
                in1=row(1, last - first),
                op=ALU.add,
            )
            if c == ROUNDS - 2:
                nc.sync.dma_start(out=out_rounds[c][:, first:last, :], in_=results[c][:, first:last, :])
            elif last == ROUND_TILES[c]:
                nc.sync.dma_start(out=out_rounds[c], in_=results[c][:])

        def transpose_out(c):
            if c == ROUNDS - 3:
                o_bank = psum_x.tile([P, ROUND_TILES[c], D_OUT], F32, tag="xt", name="o_bank")
            else:
                o_bank = psum_o.tile([P, ROUND_TILES[c], D_OUT], F32, tag="o_bank", name="o_bank")
            for j in range(ROUND_TILES[c]):
                nc.tensor.transpose(o_bank[:, j, :], outT[c][:, j, :], identity[:])
            out_banks[c] = o_bank

        def store_out(c):
            result = result_pool.tile([P, ROUND_TILES[c], D_OUT], F32, name="result")
            nc.scalar.copy(out=result[:], in_=out_banks[c][:])
            queue = nc.scalar if c == ROUNDS - 3 else nc.sync
            queue.dma_start(out=out_rounds[c], in_=result[:])

        idle_bank = psum_h.tile([P, P], F32, tag="hT", name="idle_bank")

        def warm_up(count):
            for i in range(count):
                nc.tensor.matmul(idle_bank[:], lhsT=ones[:], rhs=ones[:], start=True, stop=True)

        warm_up(WARM_UPS[0])
        s2_bank = psum_z.tile([P, PACK], F32, tag="z", name="s2_bank")
        for t in range(PACK):
            u, e = divmod(t, 2)
            first_k = 2 * D_OUT + 2 * P * u + e
            nc.tensor.matmul(
                s2_bank[:, t : t + 1],
                lhsT=row_bf[:, first_k : first_k + 2 * P - 1 : 2],
                rhs=ones[:, 0:1],
                start=True,
                stop=True,
            )
        s2_word = const.tile([P, PACK], BF16)
        nc.vector.tensor_copy(out=s2_word[:], in_=s2_bank[:])
        transpose_x(0, 0)
        rows_columns_bank = psum_o.tile([P, 2 * D_OUT + 2], F32, tag="o_bank", name="rows_columns_bank")
        nc.tensor.matmul(
            rows_columns_bank[:, : 2 * D_OUT], lhsT=ones[:], rhs=row_bf[:, : 2 * D_OUT], start=True, stop=True
        )
        for i in range(2):
            nc.tensor.matmul(
                rows_columns_bank[:, 2 * D_OUT + i : 2 * D_OUT + i + 1],
                lhsT=row_bf[:, i * D_OUT : (i + 1) * D_OUT],
                rhs=ones[:, 0:1],
                start=True,
                stop=True,
            )
        warm_up(WARM_UPS[1])
        v_grouped = const.tile([P, PACK, P, PACK], BF16, align_bytes=64)
        v_codes = const.tile([P, R], U32, align_bytes=64)
        v_scales = const.tile([P, R], U8, align_bytes=64)
        for s in range(PACK):
            if s == 2:
                scale_x(0)
            if s == 3:
                quantise_a(0)
            columns = slice(s * P, (s + 1) * P)
            nc.scalar.activation(
                out=v_grouped[:, s, :, :].rearrange("p (c i) t -> p c t i", i=PACK),
                in_=v_raw[:].rearrange("p t (c i s) -> p s c t i", i=PACK, s=PACK)[:, s, :, :, :],
                func=ACT.Sign,
            )
            nc.vector.quantize_mx(
                out=v_codes[:, columns].bitcast(FP8X4),
                scales=v_scales[:, columns],
                in_=v_grouped[:, s, :, :].rearrange("p m t -> p (m t)"),
            )

        s1_bias = const.tile([P, 2 * D_OUT + 2], F32)
        nc.scalar.copy(out=s1_bias[:], in_=rows_columns_bank[:])
        s1_bias_rows = s1_bias[:, : 2 * D_OUT]
        s1_column = s1_bias[:, 2 * D_OUT : 2 * D_OUT + 1]
        bias_column = s1_bias[:, 2 * D_OUT + 1 :]
        transpose_x(1, 0)
        transpose_x(1, 2)
        u_words = u_raw[:].bitcast(F32).rearrange("o (m u) -> o u m", u=HALVES)
        uT = psum_z.tile([P, HALVES, D_OUT], F32, tag="z", name="uT")
        for u in range(HALVES):
            nc.tensor.transpose(uT[:, u, :], u_words[:, u, :], identity[:])
        warm_up(WARM_UPS[2])
        u_grouped = const.tile([P, D_OUT, HALVES, 2], BF16, align_bytes=64)
        nc.scalar.activation(
            out=u_grouped[:],
            in_=uT[:].bitcast(BF16).rearrange("m u (o e) -> m o u e", e=2),
            func=ACT.Sign,
        )
        u_codes = const.tile([P, D_OUT], U32, align_bytes=64)
        u_scales = const.tile([P, D_OUT], U8, align_bytes=64)

        def quantise_u():
            nc.vector.quantize_mx(
                out=u_codes[:].bitcast(FP8X4),
                scales=u_scales[:],
                in_=u_grouped[:].rearrange("m o u e -> m (o u e)"),
            )

        scale_x(1)
        for n in range(ROUNDS - 2):
            last = ROUND_TILES[n] - 1
            new_h(n)
            first_matmul(n, 0, last)
            if live(n - 2) and direct(n - 2):
                second_matmul(n - 2)
            first_matmul(n, last, last + 1)
            if transposed(n - 2):
                second_matmul(n - 2)
            transpose_x(n + 2, 0)
            if transposed(n - 3):
                transpose_out(n - 3)
            transpose_x(n + 2, 2)
            copy_h(n, 0, last, nc.scalar.copy)
            if transposed(n - 2):
                scale_zT(n - 2)
            copy_h(n, last, last + 1, nc.scalar.copy)
            if transposed(n - 3):
                store_out(n - 3)
            if n == 0:
                quantise_a(1, 2)
            elif n == 1:
                quantise_a(2)
                quantise_h(0)
            else:
                quantise_h(n - 1)
                quantise_a(n + 1)
            if live(n - 2) and direct(n - 2):
                scale_z(n - 2, 0, 2)
                add_bias(n - 2, 0, 2, nc.gpsimd)
            if live(n - 3) and direct(n - 3):
                scale_z(n - 3, 2, 4)
                add_bias(n - 3, 2, 4, nc.gpsimd)
            scale_x(n + 2)
            if n == 0:
                quantise_u()

        new_h(ROUNDS - 2)
        first_matmul(ROUNDS - 2, 0, 3)
        second_matmul(ROUNDS - 4)
        first_matmul(ROUNDS - 2, 3, 4)
        transpose_out(ROUNDS - 5)
        copy_h(ROUNDS - 2, 0, 1, nc.vector.tensor_copy)
        copy_h(ROUNDS - 2, 1, 4, nc.scalar.copy)
        quantise_a(ROUNDS - 1)
        new_h(ROUNDS - 1)
        first_matmul(ROUNDS - 1, 0, 2)
        copy_h(ROUNDS - 1, 0, 2, nc.scalar.copy)
        quantise_h(ROUNDS - 3)
        scale_z(ROUNDS - 4, 0, 4)
        second_matmul(ROUNDS - 3)
        store_out(ROUNDS - 5)
        scale_zT(ROUNDS - 3)
        quantise_h(ROUNDS - 2)
        add_bias(ROUNDS - 4, 0, 4, nc.vector)
        quantise_h(ROUNDS - 1)
        second_matmul(ROUNDS - 2)
        second_matmul(ROUNDS - 1)
        transpose_out(ROUNDS - 3)
        store_out(ROUNDS - 3)
        scale_z(ROUNDS - 2, 0, 2)
        scale_z(ROUNDS - 2, 2, 4)
        add_bias(ROUNDS - 2, 0, 2, nc.vector)
        scale_z(ROUNDS - 1, 0, 2)
        add_bias(ROUNDS - 2, 2, 4, nc.vector)
        add_bias(ROUNDS - 1, 0, 2, nc.vector)
